import numpy as np
import ml_dtypes


def mxq(x, axis, fmt="e4m3"):
    dtype, down = {"e4m3": (ml_dtypes.float8_e4m3fn, 7), "e5m2": (ml_dtypes.float8_e5m2, 14)}[fmt]
    v = np.moveaxis(np.asarray(x, np.float32).astype(ml_dtypes.bfloat16).astype(np.float64), axis, -1)
    blocks = v.reshape(v.shape[:-1] + (-1, 32))
    amax = np.abs(blocks).max(-1, keepdims=True)
    byte = np.maximum(np.where(amax > 0, np.frexp(amax)[1] - 1 + 127, 0) - down, 1)
    scale = np.exp2(byte - 127.0)
    codes = (blocks / scale).astype(np.float32).astype(dtype).astype(np.float64)
    return np.moveaxis((codes * scale).reshape(v.shape), -1, axis)


WIDE = False


def mx_kscale(k):
    if not WIDE:
        return np.ones(k)
    levels = np.array([10, -10, 5, -5, 0])
    a = np.random.permutation(np.resize(levels, k // 512 * 4)).reshape(k // 512, 4)
    idx = np.arange(k)
    return np.exp2(a[idx // 512, idx % 128 // 32])


BF16 = ml_dtypes.bfloat16


def bf(x):
    return np.asarray(x, np.float32).astype(BF16)


def f64(x):
    return np.asarray(x).astype(np.float64)


N, M, P, D = 4096, 1024, 1024, 16
LN_EPS = 1e-5
LENGTHSCALE = 1.0
INPUT_LB, INPUT_UB = -2.0, 2.0


def setup_inputs():
    s = mx_kscale(M)
    r = s.max() / s
    c = np.random.standard_normal(D)
    c = (c - c.mean()) / c.std()
    x = c + np.random.standard_normal((N, D)) * 1.6 / D
    z = c + np.random.uniform(INPUT_LB, INPUT_UB, (M, D)) * 1.6 / D
    z[:, 0] += np.log(r) * LENGTHSCALE
    g = np.random.standard_normal((M, P)) * 4.0 / np.sqrt(M)
    w = np.triu(g) + 0.1 * np.tril(g, -1) + np.eye(M, P)
    return {"x": bf(x), "design_points": bf(z), "chol_inv": bf(w * r[:, None])}


def reference(x, design_points, chol_inv):
    x, z = f64(x), f64(design_points)
    mean = np.mean(x, axis=-1, keepdims=True)
    var = np.mean(np.square(x - mean), axis=-1, keepdims=True)
    xn = (x - mean) / np.sqrt(var + LN_EPS)
    l1 = np.zeros((N, M))
    for d in range(D):
        l1 = l1 + np.abs(xn[:, d, None] - z[None, :, d])
    kmat = np.exp(-l1 / LENGTHSCALE)
    return mxq(kmat, 1, "e4m3") @ mxq(f64(chol_inv), 0, "e4m3")

@@ -1,0 +1,166 @@
+from contextlib import ExitStack
+
+import concourse.mybir as mybir
+from concourse.masks import make_identity
+
+F32 = mybir.dt.float32
+BF16 = mybir.dt.bfloat16
+U32 = mybir.dt.uint32
+U8 = mybir.dt.uint8
+FP8X4 = mybir.dt.float8_e4m3fn_x4
+ALU = mybir.AluOpType
+ACT = mybir.ActivationFunctionType
+AX = mybir.AxisListType
+
+P = 128
+N, M, COLS, D = 4096, 1024, 1024, 16
+NB = N // P
+PACK = 4
+K_PASS = P * PACK
+PASSES = M // K_PASS
+N_TILE = 512
+LN_EPS = 1e-5
+FLOPS = 2 * N * M * COLS
+
+ABS_D = (0, 1, 2, 3, 4, 5)
+MAX_LO = 6
+MAX_GROUPS = ((6, 8), (8, 10), (10, 12), (12, 14), (14, 16))
+
+
+def tile_tmk_kernel(tc, x, design_points, chol_inv, out):
+    nc = tc.nc
+    out_blocks = out.rearrange("(p b) c -> b p c", b=NB)
+    with ExitStack() as stack:
+        keep = stack.enter_context(tc.tile_pool(name="keep", bufs=1))
+
+        ident = keep.tile([P, P], F32)
+        make_identity(nc, ident[:])
+        zb = keep.tile([P, D, M], BF16)
+        zr = keep.tile([P, M], F32)
+        w_codes = keep.tile([P, PASSES, COLS], U32, align_bytes=64)
+        w_scales = keep.tile([P, PASSES, COLS], U8, align_bytes=64)
+        xn = keep.tile([P, NB, D], F32)
+        hneg = keep.tile([P, NB, D], F32)
+        shift = keep.tile([P, len(MAX_GROUPS), NB], F32)
+
+        with tc.tile_pool(name="setup", bufs=1) as setup:
+            x_raw = setup.tile([P, NB, D], BF16)
+            nc.sync.dma_start(out=x_raw[:], in_=x.rearrange("(p b) d -> p b d", b=NB))
+            z_raw = setup.tile([P, M * D], BF16)
+            nc.sync.dma_start(out=z_raw[:], in_=design_points.rearrange("m d -> (m d)").partition_broadcast(P))
+
+            xf = setup.tile([P, NB, D], F32)
+            nc.vector.tensor_copy(out=xf[:], in_=x_raw[:])
+            mean = setup.tile([P, NB], F32)
+            nc.vector.tensor_reduce(out=mean[:], in_=xf[:], axis=AX.X, op=ALU.add)
+            nc.vector.tensor_scalar_mul(out=mean[:], in0=mean[:], scalar1=1.0 / D)
+            xc = setup.tile([P, NB, D], F32)
+            nc.vector.tensor_tensor(out=xc[:], in0=xf[:], in1=mean[:].unsqueeze(2).to_broadcast([P, NB, D]), op=ALU.subtract)
+            sq = setup.tile([P, NB, D], F32)
+            nc.vector.tensor_tensor(out=sq[:], in0=xc[:], in1=xc[:], op=ALU.mult)
+            var = setup.tile([P, NB], F32)
+            nc.vector.tensor_reduce(out=var[:], in_=sq[:], axis=AX.X, op=ALU.add)
+            nc.vector.tensor_scalar(out=var[:], in0=var[:], scalar1=1.0 / D, scalar2=LN_EPS, op0=ALU.mult, op1=ALU.add)
+            std = setup.tile([P, NB], F32)
+            nc.scalar.activation(out=std[:], in_=var[:], func=ACT.Sqrt)
+            rstd = setup.tile([P, NB], F32)
+            nc.vector.reciprocal(out=rstd[:], in_=std[:])
+            nt = setup.tile([P, NB], F32)
+            nc.vector.tensor_tensor(out=nt[:], in0=rstd[:], in1=rstd[:], op=ALU.mult)
+            nc.vector.tensor_tensor(out=nt[:], in0=nt[:], in1=var[:], op=ALU.mult)
+            nc.vector.tensor_scalar(out=nt[:], in0=nt[:], scalar1=-0.5, scalar2=1.5, op0=ALU.mult, op1=ALU.add)
+            nc.vector.tensor_tensor(out=rstd[:], in0=rstd[:], in1=nt[:], op=ALU.mult)
+            nc.vector.tensor_tensor(out=xn[:], in0=xc[:], in1=rstd[:].unsqueeze(2).to_broadcast([P, NB, D]), op=ALU.mult)
+            nc.vector.tensor_scalar_mul(out=hneg[:], in0=xn[:], scalar1=-0.5)
+            for j, (lo, hi) in enumerate(MAX_GROUPS):
+                nc.vector.tensor_reduce(out=shift[:, j, :], in_=hneg[:, :, lo:hi], axis=AX.X, op=ALU.add)
+
+            z_view = z_raw[:].rearrange("p (c q t d) -> p d c t q", c=PASSES, q=P, t=PACK, d=D)
+            for d in range(D):
+                dst = zb[:, d, :].rearrange("p (c t q) -> p c t q", c=PASSES, t=PACK)
+                if d % 2 == 0:
+                    nc.scalar.copy(out=dst, in_=z_view[:, d])
+                else:
+                    nc.vector.tensor_copy(out=dst, in_=z_view[:, d])
+            z_sum = setup.tile([P, M], F32)
+            nc.vector.tensor_reduce(
+                out=z_sum[:], in_=z_raw[:].rearrange("p (m d) -> p m d", d=D)[:, :, MAX_LO:D], axis=AX.X, op=ALU.add
+            )
+            nc.vector.tensor_scalar_mul(
+                out=zr[:].rearrange("p (c t q) -> p c t q", c=PASSES, t=PACK),
+                in0=z_sum[:].rearrange("p (c q t) -> p c t q", c=PASSES, t=PACK),
+                scalar1=-0.5,
+            )
+
+            for c in range(PASSES):
+                w_raw = setup.tile([P, PACK, COLS], BF16, tag="w_raw")
+                nc.sync.dma_start(
+                    out=w_raw[:], in_=chol_inv[c * K_PASS : (c + 1) * K_PASS, :].rearrange("(p j) w -> p j w", j=PACK)
+                )
+                w_grouped = setup.tile([P, COLS, PACK], BF16, tag="w_grouped", align_bytes=64)
+                nc.vector.tensor_copy(out=w_grouped[:], in_=w_raw[:].rearrange("p j w -> p w j"))
+                nc.vector.quantize_mx(
+                    out=w_codes[:, c, :].bitcast(FP8X4),
+                    scales=w_scales[:, c, :],
+                    in_=w_grouped[:].rearrange("p w j -> p (w j)"),
+                )
+
+        terms = stack.enter_context(tc.tile_pool(name="terms", bufs=22))
+        work = stack.enter_context(tc.tile_pool(name="work", bufs=3))
+        q_psum = stack.enter_context(tc.psum_pool(name="q_psum", bufs=4))
+        o_psum = stack.enter_context(tc.psum_pool(name="o_psum", bufs=4))
+
+        for b in range(NB):
+            parts = [zr]
+            for d in ABS_D:
+                ta = terms.tile([P, M], F32, tag="term", name="ta")
+                nc.scalar.activation(out=ta[:], in_=zb[:, d, :], func=ACT.Abs, bias=hneg[:, b, d : d + 1], scale=0.5)
+                parts.append(ta)
+            for j, (lo, hi) in enumerate(MAX_GROUPS):
+                tm = terms.tile([P, M], F32, tag="term", name="tm")
+                nc.vector.tensor_scalar(
+                    out=tm[:], in0=zb[:, lo, :], scalar1=xn[:, b, lo : lo + 1], scalar2=shift[:, j, b : b + 1],
+                    op0=ALU.max, op1=ALU.add,
+                )
+                for d in range(lo + 1, hi):
+                    nc.vector.scalar_tensor_tensor(
+                        out=tm[:], in0=zb[:, d, :], scalar=xn[:, b, d : d + 1], in1=tm[:], op0=ALU.max, op1=ALU.add
+                    )
+                parts.append(tm)
+
+            k_grouped = work.tile([P, PASSES, P, PACK], BF16, align_bytes=64)
+            for c in range(PASSES):
+                half_l1 = q_psum.tile([P, PACK, P], F32)
+                for t in range(PACK):
+                    lo = c * K_PASS + t * P
+                    for i, part in enumerate(parts):
+                        nc.tensor.matmul(
+                            out=half_l1[:, t, :], lhsT=part[:, lo : lo + P], rhs=ident[:], is_transpose=True,
+                            start=(i == 0), stop=(i == len(parts) - 1),
+                        )
+                nc.scalar.activation(
+                    out=k_grouped[:, c, :, :], in_=half_l1[:].rearrange("p t n -> p n t"), func=ACT.Exp, scale=-2.0
+                )
+            k_codes = work.tile([P, PASSES * P], U32, align_bytes=64)
+            k_scales = work.tile([P, PASSES * P], U8, align_bytes=64)
+            nc.vector.quantize_mx(
+                out=k_codes[:].bitcast(FP8X4), scales=k_scales[:], in_=k_grouped[:].rearrange("p c n t -> p (c n t)")
+            )
+            result = work.tile([P, COLS], F32)
+            for h in range(COLS // N_TILE):
+                acc = o_psum.tile([P, N_TILE], F32)
+                for c in range(PASSES):
+                    nc.tensor.matmul_mx(
+                        out=acc[:],
+                        lhsT=k_codes[:, c * P : (c + 1) * P].bitcast(FP8X4),
+                        lhsT_scale=k_scales[:, c * P : (c + 1) * P],
+                        rhs=w_codes[:, c, h * N_TILE : (h + 1) * N_TILE].bitcast(FP8X4),
+                        rhs_scale=w_scales[:, c, h * N_TILE : (h + 1) * N_TILE],
+                        start=(c == 0),
+                        stop=(c == PASSES - 1),
+                    )
+                if h == 0:
+                    nc.scalar.copy(out=result[:, h * N_TILE : (h + 1) * N_TILE], in_=acc[:])
+                else:
+                    nc.vector.tensor_copy(out=result[:, h * N_TILE : (h + 1) * N_TILE], in_=acc[:])
+            nc.sync.dma_start(out=out_blocks[b], in_=result[:])

@@ -18,13 +18,13 @@ NB = N // P
 PACK = 4
 K_PASS = P * PACK
 PASSES = M // K_PASS
+CT = PASSES * PACK
 N_TILE = 512
 LN_EPS = 1e-5
 FLOPS = 2 * N * M * COLS
 
-ABS_D = (0, 1, 2, 3, 4, 5)
-MAX_LO = 6
-MAX_GROUPS = ((6, 8), (8, 10), (10, 12), (12, 14), (14, 16))
+N_RELU = 7
+ADDS = ((7, 8), (9, 10), (11,), (12,), (13,), (14,), (15,))
 
 
 def tile_tmk_kernel(tc, x, design_points, chol_inv, out):
@@ -32,105 +32,106 @@ def tile_tmk_kernel(tc, x, design_points, chol_inv, out):
     out_blocks = out.rearrange("(p b) c -> b p c", b=NB)
     with ExitStack() as stack:
         keep = stack.enter_context(tc.tile_pool(name="keep", bufs=1))
+        setup = stack.enter_context(tc.tile_pool(name="setup", bufs=1))
+        terms = stack.enter_context(tc.tile_pool(name="terms", bufs=24))
+        work = stack.enter_context(tc.tile_pool(name="work", bufs=3))
+        q_psum = stack.enter_context(tc.psum_pool(name="q_psum", bufs=4))
+        o_psum = stack.enter_context(tc.psum_pool(name="o_psum", bufs=4))
+
+        x_raw = setup.tile([P, NB, D], BF16)
+        nc.sync.dma_start(out=x_raw[:], in_=x.rearrange("(p b) d -> p b d", b=NB))
+        z_sb = setup.tile([P, PASSES, PACK, D], BF16)
+        nc.sync.dma_start(out=z_sb[:], in_=design_points.rearrange("(c q t) d -> q c t d", c=PASSES, t=PACK))
+        w_raws = []
+        for c in range(PASSES):
+            w_raw = setup.tile([P, PACK, COLS], BF16, name="w_raw%d" % c)
+            nc.sync.dma_start(
+                out=w_raw[:], in_=chol_inv[c * K_PASS : (c + 1) * K_PASS, :].rearrange("(p j) w -> p j w", j=PACK)
+            )
+            w_raws.append(w_raw)
 
         ident = keep.tile([P, P], F32)
         make_identity(nc, ident[:])
+        ident_bf = keep.tile([P, P], BF16)
+        make_identity(nc, ident_bf[:])
         zb = keep.tile([P, D, M], BF16)
         zr = keep.tile([P, M], F32)
         w_codes = keep.tile([P, PASSES, COLS], U32, align_bytes=64)
         w_scales = keep.tile([P, PASSES, COLS], U8, align_bytes=64)
         xn = keep.tile([P, NB, D], F32)
-        hneg = keep.tile([P, NB, D], F32)
-        shift = keep.tile([P, len(MAX_GROUPS), NB], F32)
 
-        with tc.tile_pool(name="setup", bufs=1) as setup:
-            x_raw = setup.tile([P, NB, D], BF16)
-            nc.sync.dma_start(out=x_raw[:], in_=x.rearrange("(p b) d -> p b d", b=NB))
-            z_raw = setup.tile([P, M * D], BF16)
-            nc.sync.dma_start(out=z_raw[:], in_=design_points.rearrange("m d -> (m d)").partition_broadcast(P))
+        xf = setup.tile([P, NB, D], F32)
+        nc.vector.tensor_copy(out=xf[:], in_=x_raw[:])
+        mean = setup.tile([P, NB], F32)
+        nc.vector.tensor_reduce(out=mean[:], in_=xf[:], axis=AX.X, op=ALU.add)
+        nc.vector.tensor_scalar_mul(out=mean[:], in0=mean[:], scalar1=1.0 / D)
+        xc = setup.tile([P, NB, D], F32)
+        nc.vector.tensor_tensor(out=xc[:], in0=xf[:], in1=mean[:].unsqueeze(2).to_broadcast([P, NB, D]), op=ALU.subtract)
+        sq = setup.tile([P, NB, D], F32)
+        nc.vector.tensor_tensor(out=sq[:], in0=xc[:], in1=xc[:], op=ALU.mult)
+        var = setup.tile([P, NB], F32)
+        nc.vector.tensor_reduce(out=var[:], in_=sq[:], axis=AX.X, op=ALU.add)
+        nc.vector.tensor_scalar(out=var[:], in0=var[:], scalar1=1.0 / D, scalar2=LN_EPS, op0=ALU.mult, op1=ALU.add)
+        std = setup.tile([P, NB], F32)
+        nc.scalar.activation(out=std[:], in_=var[:], func=ACT.Sqrt)
+        rstd = setup.tile([P, NB], F32)
+        nc.vector.reciprocal(out=rstd[:], in_=std[:])
+        nt = setup.tile([P, NB], F32)
+        nc.vector.tensor_tensor(out=nt[:], in0=rstd[:], in1=rstd[:], op=ALU.mult)
+        nc.vector.tensor_tensor(out=nt[:], in0=nt[:], in1=var[:], op=ALU.mult)
+        nc.vector.tensor_scalar(out=nt[:], in0=nt[:], scalar1=-0.5, scalar2=1.5, op0=ALU.mult, op1=ALU.add)
+        nc.vector.tensor_tensor(out=rstd[:], in0=rstd[:], in1=nt[:], op=ALU.mult)
+        nc.vector.tensor_tensor(out=xn[:], in0=xc[:], in1=rstd[:].unsqueeze(2).to_broadcast([P, NB, D]), op=ALU.mult)
 
-            xf = setup.tile([P, NB, D], F32)
-            nc.vector.tensor_copy(out=xf[:], in_=x_raw[:])
-            mean = setup.tile([P, NB], F32)
-            nc.vector.tensor_reduce(out=mean[:], in_=xf[:], axis=AX.X, op=ALU.add)
-            nc.vector.tensor_scalar_mul(out=mean[:], in0=mean[:], scalar1=1.0 / D)
-            xc = setup.tile([P, NB, D], F32)
-            nc.vector.tensor_tensor(out=xc[:], in0=xf[:], in1=mean[:].unsqueeze(2).to_broadcast([P, NB, D]), op=ALU.subtract)
-            sq = setup.tile([P, NB, D], F32)
-            nc.vector.tensor_tensor(out=sq[:], in0=xc[:], in1=xc[:], op=ALU.mult)
-            var = setup.tile([P, NB], F32)
-            nc.vector.tensor_reduce(out=var[:], in_=sq[:], axis=AX.X, op=ALU.add)
-            nc.vector.tensor_scalar(out=var[:], in0=var[:], scalar1=1.0 / D, scalar2=LN_EPS, op0=ALU.mult, op1=ALU.add)
-            std = setup.tile([P, NB], F32)
-            nc.scalar.activation(out=std[:], in_=var[:], func=ACT.Sqrt)
-            rstd = setup.tile([P, NB], F32)
-            nc.vector.reciprocal(out=rstd[:], in_=std[:])
-            nt = setup.tile([P, NB], F32)
-            nc.vector.tensor_tensor(out=nt[:], in0=rstd[:], in1=rstd[:], op=ALU.mult)
-            nc.vector.tensor_tensor(out=nt[:], in0=nt[:], in1=var[:], op=ALU.mult)
-            nc.vector.tensor_scalar(out=nt[:], in0=nt[:], scalar1=-0.5, scalar2=1.5, op0=ALU.mult, op1=ALU.add)
-            nc.vector.tensor_tensor(out=rstd[:], in0=rstd[:], in1=nt[:], op=ALU.mult)
-            nc.vector.tensor_tensor(out=xn[:], in0=xc[:], in1=rstd[:].unsqueeze(2).to_broadcast([P, NB, D]), op=ALU.mult)
-            nc.vector.tensor_scalar_mul(out=hneg[:], in0=xn[:], scalar1=-0.5)
-            for j, (lo, hi) in enumerate(MAX_GROUPS):
-                nc.vector.tensor_reduce(out=shift[:, j, :], in_=hneg[:, :, lo:hi], axis=AX.X, op=ALU.add)
-
-            z_view = z_raw[:].rearrange("p (c q t d) -> p d c t q", c=PASSES, q=P, t=PACK, d=D)
-            for d in range(D):
-                dst = zb[:, d, :].rearrange("p (c t q) -> p c t q", c=PASSES, t=PACK)
-                if d % 2 == 0:
-                    nc.scalar.copy(out=dst, in_=z_view[:, d])
-                else:
-                    nc.vector.tensor_copy(out=dst, in_=z_view[:, d])
-            z_sum = setup.tile([P, M], F32)
-            nc.vector.tensor_reduce(
-                out=z_sum[:], in_=z_raw[:].rearrange("p (m d) -> p m d", d=D)[:, :, MAX_LO:D], axis=AX.X, op=ALU.add
-            )
-            nc.vector.tensor_scalar_mul(
-                out=zr[:].rearrange("p (c t q) -> p c t q", c=PASSES, t=PACK),
-                in0=z_sum[:].rearrange("p (c q t) -> p c t q", c=PASSES, t=PACK),
-                scalar1=-0.5,
-            )
-
+        for d in range(D):
+            plane = q_psum.tile([P, M], BF16, tag="q", name="plane")
             for c in range(PASSES):
-                w_raw = setup.tile([P, PACK, COLS], BF16, tag="w_raw")
-                nc.sync.dma_start(
-                    out=w_raw[:], in_=chol_inv[c * K_PASS : (c + 1) * K_PASS, :].rearrange("(p j) w -> p j w", j=PACK)
-                )
+                for t in range(PACK):
+                    lo = c * K_PASS + t * P
+                    nc.tensor.transpose(plane[:, lo : lo + P], z_sb[:, c, t, d : d + 1].to_broadcast([P, P]), ident_bf[:])
+            if d < N_RELU:
+                nc.scalar.copy(out=zb[:, d, :], in_=plane[:])
+            else:
+                nc.vector.tensor_copy(out=zb[:, d, :], in_=plane[:])
+        z_lo = setup.tile([P, PASSES, PACK], F32)
+        nc.vector.tensor_reduce(out=z_lo[:], in_=z_sb[:, :, :, 0:N_RELU], axis=AX.X, op=ALU.add)
+        z_hi = setup.tile([P, PASSES, PACK], F32)
+        nc.vector.tensor_reduce(out=z_hi[:], in_=z_sb[:, :, :, N_RELU:D], axis=AX.X, op=ALU.add)
+        z_rest = setup.tile([P, PASSES, PACK], F32)
+        nc.vector.tensor_tensor(out=z_rest[:], in0=z_lo[:], in1=z_hi[:], op=ALU.subtract)
+        nc.vector.tensor_scalar_mul(out=z_rest[:], in0=z_rest[:], scalar1=0.5)
+        for c in range(PASSES):
+            rest = q_psum.tile([P, PACK, P], F32, tag="q", name="rest")
+            for t in range(PACK):
+                nc.tensor.transpose(rest[:, t, :], z_rest[:, c, t : t + 1].to_broadcast([P, P]), ident[:])
+            nc.vector.tensor_copy(out=zr[:, c * K_PASS : (c + 1) * K_PASS], in_=rest[:].rearrange("p t q -> p (t q)"))
+
+        def quantise_weights():
+            for c in range(PASSES):
                 w_grouped = setup.tile([P, COLS, PACK], BF16, tag="w_grouped", align_bytes=64)
-                nc.vector.tensor_copy(out=w_grouped[:], in_=w_raw[:].rearrange("p j w -> p w j"))
+                nc.vector.tensor_copy(out=w_grouped[:], in_=w_raws[c][:].rearrange("p j w -> p w j"))
                 nc.vector.quantize_mx(
                     out=w_codes[:, c, :].bitcast(FP8X4),
                     scales=w_scales[:, c, :],
                     in_=w_grouped[:].rearrange("p w j -> p (w j)"),
                 )
 
-        terms = stack.enter_context(tc.tile_pool(name="terms", bufs=22))
-        work = stack.enter_context(tc.tile_pool(name="work", bufs=3))
-        q_psum = stack.enter_context(tc.psum_pool(name="q_psum", bufs=4))
-        o_psum = stack.enter_context(tc.psum_pool(name="o_psum", bufs=4))
-
-        for b in range(NB):
+        def make_terms(b):
             parts = [zr]
-            for d in ABS_D:
-                ta = terms.tile([P, M], F32, tag="term", name="ta")
-                nc.scalar.activation(out=ta[:], in_=zb[:, d, :], func=ACT.Abs, bias=hneg[:, b, d : d + 1], scale=0.5)
-                parts.append(ta)
-            for j, (lo, hi) in enumerate(MAX_GROUPS):
-                tm = terms.tile([P, M], F32, tag="term", name="tm")
-                nc.vector.tensor_scalar(
-                    out=tm[:], in0=zb[:, lo, :], scalar1=xn[:, b, lo : lo + 1], scalar2=shift[:, j, b : b + 1],
-                    op0=ALU.max, op1=ALU.add,
-                )
-                for d in range(lo + 1, hi):
+            for i in range(N_RELU):
+                part = terms.tile([P, M], F32, tag="term", name="part")
+                nc.scalar.activation(out=part[:], in_=zb[:, i, :], func=ACT.Relu, bias=xn[:, b, i : i + 1], scale=-1.0)
+                for d in ADDS[i]:
                     nc.vector.scalar_tensor_tensor(
-                        out=tm[:], in0=zb[:, d, :], scalar=xn[:, b, d : d + 1], in1=tm[:], op0=ALU.max, op1=ALU.add
+                        out=part[:], in0=zb[:, d, :], scalar=xn[:, b, d : d + 1], in1=part[:], op0=ALU.max, op1=ALU.add
                     )
-                parts.append(tm)
+                parts.append(part)
+            return parts
 
+        def finish(b, parts):
             k_grouped = work.tile([P, PASSES, P, PACK], BF16, align_bytes=64)
             for c in range(PASSES):
-                half_l1 = q_psum.tile([P, PACK, P], F32)
+                half_l1 = q_psum.tile([P, PACK, P], F32, tag="q", name="half_l1")
                 for t in range(PACK):
                     lo = c * K_PASS + t * P
                     for i, part in enumerate(parts):
@@ -159,8 +160,14 @@ def tile_tmk_kernel(tc, x, design_points, chol_inv, out):
                         start=(c == 0),
                         stop=(c == PASSES - 1),
                     )
-                if h == 0:
-                    nc.scalar.copy(out=result[:, h * N_TILE : (h + 1) * N_TILE], in_=acc[:])
-                else:
-                    nc.vector.tensor_copy(out=result[:, h * N_TILE : (h + 1) * N_TILE], in_=acc[:])
+                nc.scalar.copy(out=result[:, h * N_TILE : (h + 1) * N_TILE], in_=acc[:])
             nc.sync.dma_start(out=out_blocks[b], in_=result[:])
+
+        made = {}
+        for b in range(NB):
+            made[b] = make_terms(b)
+            if b == 0:
+                quantise_weights()
+            if b >= 1:
+                finish(b - 1, made[b - 1])
+        finish(NB - 1, made[NB - 1])

@@ -23,8 +23,10 @@ N_TILE = 512
 LN_EPS = 1e-5
 FLOPS = 2 * N * M * COLS
 
-N_RELU = 7
-ADDS = ((7, 8), (9, 10), (11,), (12,), (13,), (14,), (15,))
+N_RELU = 6
+CHAINS = ((6, 9, 12), (7, 10, 13), (8, 11, 14, 15))
+PLANE_ORDER = (0, 6, 1, 7, 2, 8, 3, 9, 4, 10, 5, 11, 12, 13, 14, 15)
+LEAD = 1
 
 
 def tile_tmk_kernel(tc, x, design_points, chol_inv, out):
@@ -33,7 +35,7 @@ def tile_tmk_kernel(tc, x, design_points, chol_inv, out):
     with ExitStack() as stack:
         keep = stack.enter_context(tc.tile_pool(name="keep", bufs=1))
         setup = stack.enter_context(tc.tile_pool(name="setup", bufs=1))
-        terms = stack.enter_context(tc.tile_pool(name="terms", bufs=24))
+        terms = stack.enter_context(tc.tile_pool(name="terms", bufs=27))
         work = stack.enter_context(tc.tile_pool(name="work", bufs=3))
         q_psum = stack.enter_context(tc.psum_pool(name="q_psum", bufs=4))
         o_psum = stack.enter_context(tc.psum_pool(name="o_psum", bufs=4))
@@ -83,7 +85,7 @@ def tile_tmk_kernel(tc, x, design_points, chol_inv, out):
         nc.vector.tensor_tensor(out=rstd[:], in0=rstd[:], in1=nt[:], op=ALU.mult)
         nc.vector.tensor_tensor(out=xn[:], in0=xc[:], in1=rstd[:].unsqueeze(2).to_broadcast([P, NB, D]), op=ALU.mult)
 
-        for d in range(D):
+        for d in PLANE_ORDER:
             plane = q_psum.tile([P, M], BF16, tag="q", name="plane")
             for c in range(PASSES):
                 for t in range(PACK):
@@ -116,58 +118,94 @@ def tile_tmk_kernel(tc, x, design_points, chol_inv, out):
                     in_=w_grouped[:].rearrange("p w j -> p (w j)"),
                 )
 
-        def make_terms(b):
-            parts = [zr]
-            for i in range(N_RELU):
-                part = terms.tile([P, M], F32, tag="term", name="part")
-                nc.scalar.activation(out=part[:], in_=zb[:, i, :], func=ACT.Relu, bias=xn[:, b, i : i + 1], scale=-1.0)
-                for d in ADDS[i]:
-                    nc.vector.scalar_tensor_tensor(
-                        out=part[:], in0=zb[:, d, :], scalar=xn[:, b, d : d + 1], in1=part[:], op0=ALU.max, op1=ALU.add
-                    )
-                parts.append(part)
-            return parts
+        def relu_term(b, d):
+            part = terms.tile([P, M], F32, tag="term", name="part")
+            nc.scalar.activation(out=part[:], in_=zb[:, d, :], func=ACT.Relu, bias=xn[:, b, d : d + 1], scale=-1.0)
+            return part
 
-        def finish(b, parts):
-            k_grouped = work.tile([P, PASSES, P, PACK], BF16, align_bytes=64)
-            for c in range(PASSES):
-                half_l1 = q_psum.tile([P, PACK, P], F32, tag="q", name="half_l1")
-                for t in range(PACK):
-                    lo = c * K_PASS + t * P
-                    for i, part in enumerate(parts):
-                        nc.tensor.matmul(
-                            out=half_l1[:, t, :], lhsT=part[:, lo : lo + P], rhs=ident[:], is_transpose=True,
-                            start=(i == 0), stop=(i == len(parts) - 1),
+        def max_terms(b):
+            chains = []
+            for chain in CHAINS:
+                part = terms.tile([P, M], F32, tag="term", name="chain")
+                d = chain[0]
+                nc.vector.tensor_scalar(out=part[:], in0=zb[:, d, :], scalar1=xn[:, b, d : d + 1], scalar2=None, op0=ALU.max)
+                chains.append(part)
+            for step in range(1, max(len(chain) for chain in CHAINS)):
+                for chain, part in zip(CHAINS, chains):
+                    if step < len(chain):
+                        d = chain[step]
+                        nc.vector.scalar_tensor_tensor(
+                            out=part[:], in0=zb[:, d, :], scalar=xn[:, b, d : d + 1], in1=part[:], op0=ALU.max, op1=ALU.add
                         )
-                nc.scalar.activation(
-                    out=k_grouped[:, c, :, :], in_=half_l1[:].rearrange("p t n -> p n t"), func=ACT.Exp, scale=-2.0
-                )
-            k_codes = work.tile([P, PASSES * P], U32, align_bytes=64)
-            k_scales = work.tile([P, PASSES * P], U8, align_bytes=64)
-            nc.vector.quantize_mx(
-                out=k_codes[:].bitcast(FP8X4), scales=k_scales[:], in_=k_grouped[:].rearrange("p c n t -> p (c n t)")
-            )
-            result = work.tile([P, COLS], F32)
-            for h in range(COLS // N_TILE):
-                acc = o_psum.tile([P, N_TILE], F32)
-                for c in range(PASSES):
-                    nc.tensor.matmul_mx(
-                        out=acc[:],
-                        lhsT=k_codes[:, c * P : (c + 1) * P].bitcast(FP8X4),
-                        lhsT_scale=k_scales[:, c * P : (c + 1) * P],
-                        rhs=w_codes[:, c, h * N_TILE : (h + 1) * N_TILE].bitcast(FP8X4),
-                        rhs_scale=w_scales[:, c, h * N_TILE : (h + 1) * N_TILE],
-                        start=(c == 0),
-                        stop=(c == PASSES - 1),
-                    )
-                nc.scalar.copy(out=result[:, h * N_TILE : (h + 1) * N_TILE], in_=acc[:])
-            nc.sync.dma_start(out=out_blocks[b], in_=result[:])
+            return chains
 
-        made = {}
-        for b in range(NB):
-            made[b] = make_terms(b)
-            if b == 0:
-                quantise_weights()
-            if b >= 1:
-                finish(b - 1, made[b - 1])
-        finish(NB - 1, made[NB - 1])
+        def sum_terms(parts, c):
+            half_l1 = q_psum.tile([P, PACK, P], F32, tag="q", name="half_l1")
+            for t in range(PACK):
+                lo = c * K_PASS + t * P
+                for i, part in enumerate(parts):
+                    nc.tensor.matmul(
+                        out=half_l1[:, t, :], lhsT=part[:, lo : lo + P], rhs=ident[:], is_transpose=(i > 0 or t == PACK - 1),
+                        start=(i == 0), stop=(i == len(parts) - 1),
+                    )
+            return half_l1
+
+        def exponential(k_grouped, half_l1, c):
+            nc.scalar.activation(
+                out=k_grouped[:, c, :, :], in_=half_l1[:].rearrange("p t n -> p n t"), func=ACT.Exp, scale=-2.0
+            )
+
+        def multiply(k_codes, k_scales, h):
+            acc = o_psum.tile([P, N_TILE], F32, name="acc")
+            for c in range(PASSES):
+                nc.tensor.matmul_mx(
+                    out=acc[:],
+                    lhsT=k_codes[:, c * P : (c + 1) * P].bitcast(FP8X4),
+                    lhsT_scale=k_scales[:, c * P : (c + 1) * P],
+                    rhs=w_codes[:, c, h * N_TILE : (h + 1) * N_TILE].bitcast(FP8X4),
+                    rhs_scale=w_scales[:, c, h * N_TILE : (h + 1) * N_TILE],
+                    start=(c == 0),
+                    stop=(c == PASSES - 1),
+                )
+            return acc
+
+        parts_of = {}
+        grouped_of = {}
+        late_half = {}
+        with tc.manual_schedule():
+            for p in range(NB + LEAD + 1):
+                q = p - LEAD
+                r = q - 1
+                if 0 <= r:
+                    exponential(grouped_of[r], late_half[r], 1)
+                    k_codes = work.tile([P, PASSES * P], U32, align_bytes=64, name="k_codes")
+                    k_scales = work.tile([P, PASSES * P], U8, align_bytes=64, name="k_scales")
+                    nc.vector.quantize_mx(
+                        out=k_codes[:].bitcast(FP8X4), scales=k_scales[:],
+                        in_=grouped_of[r][:].rearrange("p c n t -> p (c n t)"),
+                    )
+                if p < NB:
+                    parts_of[p] = [zr] + max_terms(p)
+                    for d in range(3):
+                        parts_of[p].append(relu_term(p, d))
+                if p == 0:
+                    quantise_weights()
+                if 0 <= q < NB:
+                    early_half = sum_terms(parts_of[q], 0)
+                if 0 <= r:
+                    acc0 = multiply(k_codes, k_scales, 0)
+                if 0 <= q < NB:
+                    grouped_of[q] = work.tile([P, PASSES, P, PACK], BF16, align_bytes=64, name="k_grouped")
+                    exponential(grouped_of[q], early_half, 0)
+                if 0 <= r:
+                    result = work.tile([P, COLS], F32, name="result")
+                    nc.scalar.copy(out=result[:, 0:N_TILE], in_=acc0[:])
+                if p < NB:
+                    for d in range(3, N_RELU):
+                        parts_of[p].append(relu_term(p, d))
+                if 0 <= q < NB:
+                    late_half[q] = sum_terms(parts_of[q], 1)
+                if 0 <= r:
+                    acc1 = multiply(k_codes, k_scales, 1)
+                    nc.scalar.copy(out=result[:, N_TILE:COLS], in_=acc1[:])
+                    nc.sync.dma_start(out=out_blocks[r], in_=result[:])

@@ -24,9 +24,8 @@ LN_EPS = 1e-5
 FLOPS = 2 * N * M * COLS
 
 N_RELU = 6
-CHAINS = ((6, 9, 12), (7, 10, 13), (8, 11, 14, 15))
+CHAINS = ((6, 8, 10, 12, 14), (7, 9, 11, 13, 15))
 PLANE_ORDER = (0, 6, 1, 7, 2, 8, 3, 9, 4, 10, 5, 11, 12, 13, 14, 15)
-LEAD = 1
 
 
 def tile_tmk_kernel(tc, x, design_points, chol_inv, out):
@@ -36,7 +35,7 @@ def tile_tmk_kernel(tc, x, design_points, chol_inv, out):
         keep = stack.enter_context(tc.tile_pool(name="keep", bufs=1))
         setup = stack.enter_context(tc.tile_pool(name="setup", bufs=1))
         terms = stack.enter_context(tc.tile_pool(name="terms", bufs=27))
-        work = stack.enter_context(tc.tile_pool(name="work", bufs=3))
+        work = stack.enter_context(tc.tile_pool(name="work", bufs=4))
         q_psum = stack.enter_context(tc.psum_pool(name="q_psum", bufs=4))
         o_psum = stack.enter_context(tc.psum_pool(name="o_psum", bufs=4))
 
@@ -123,21 +122,19 @@ def tile_tmk_kernel(tc, x, design_points, chol_inv, out):
             nc.scalar.activation(out=part[:], in_=zb[:, d, :], func=ACT.Relu, bias=xn[:, b, d : d + 1], scale=-1.0)
             return part
 
-        def max_terms(b):
-            chains = []
-            for chain in CHAINS:
-                part = terms.tile([P, M], F32, tag="term", name="chain")
-                d = chain[0]
-                nc.vector.tensor_scalar(out=part[:], in0=zb[:, d, :], scalar1=xn[:, b, d : d + 1], scalar2=None, op0=ALU.max)
-                chains.append(part)
-            for step in range(1, max(len(chain) for chain in CHAINS)):
-                for chain, part in zip(CHAINS, chains):
-                    if step < len(chain):
-                        d = chain[step]
-                        nc.vector.scalar_tensor_tensor(
-                            out=part[:], in0=zb[:, d, :], scalar=xn[:, b, d : d + 1], in1=part[:], op0=ALU.max, op1=ALU.add
-                        )
-            return chains
+        def chain_step(b, chains, step):
+            for j, chain in enumerate(CHAINS):
+                if step >= len(chain):
+                    continue
+                d = chain[step]
+                if step == 0:
+                    part = terms.tile([P, M], F32, tag="term", name="chain")
+                    nc.vector.tensor_scalar(out=part[:], in0=zb[:, d, :], scalar1=xn[:, b, d : d + 1], scalar2=None, op0=ALU.max)
+                    chains.append(part)
+                else:
+                    nc.vector.scalar_tensor_tensor(
+                        out=chains[j][:], in0=zb[:, d, :], scalar=xn[:, b, d : d + 1], in1=chains[j][:], op0=ALU.max, op1=ALU.add
+                    )
 
         def sum_terms(parts, c):
             half_l1 = q_psum.tile([P, PACK, P], F32, tag="q", name="half_l1")
@@ -145,67 +142,71 @@ def tile_tmk_kernel(tc, x, design_points, chol_inv, out):
                 lo = c * K_PASS + t * P
                 for i, part in enumerate(parts):
                     nc.tensor.matmul(
-                        out=half_l1[:, t, :], lhsT=part[:, lo : lo + P], rhs=ident[:], is_transpose=(i > 0 or t == PACK - 1),
+                        out=half_l1[:, t, :], lhsT=part[:, lo : lo + P], rhs=ident[:], is_transpose=True,
                         start=(i == 0), stop=(i == len(parts) - 1),
                     )
             return half_l1
 
-        def exponential(k_grouped, half_l1, c):
-            nc.scalar.activation(
-                out=k_grouped[:, c, :, :], in_=half_l1[:].rearrange("p t n -> p n t"), func=ACT.Exp, scale=-2.0
-            )
-
-        def multiply(k_codes, k_scales, h):
-            acc = o_psum.tile([P, N_TILE], F32, name="acc")
-            for c in range(PASSES):
-                nc.tensor.matmul_mx(
-                    out=acc[:],
-                    lhsT=k_codes[:, c * P : (c + 1) * P].bitcast(FP8X4),
-                    lhsT_scale=k_scales[:, c * P : (c + 1) * P],
-                    rhs=w_codes[:, c, h * N_TILE : (h + 1) * N_TILE].bitcast(FP8X4),
-                    rhs_scale=w_scales[:, c, h * N_TILE : (h + 1) * N_TILE],
-                    start=(c == 0),
-                    stop=(c == PASSES - 1),
-                )
-            return acc
-
-        parts_of = {}
+        chains_of = {}
+        relus_of = {}
+        half_of = {}
         grouped_of = {}
-        late_half = {}
+        codes_of = {}
+        acc_of = {}
+        result_of = {}
+        last = PASSES * NB
         with tc.manual_schedule():
-            for p in range(NB + LEAD + 1):
-                q = p - LEAD
-                r = q - 1
-                if 0 <= r:
-                    exponential(grouped_of[r], late_half[r], 1)
-                    k_codes = work.tile([P, PASSES * P], U32, align_bytes=64, name="k_codes")
-                    k_scales = work.tile([P, PASSES * P], U8, align_bytes=64, name="k_scales")
-                    nc.vector.quantize_mx(
-                        out=k_codes[:].bitcast(FP8X4), scales=k_scales[:],
-                        in_=grouped_of[r][:].rearrange("p c n t -> p (c n t)"),
+            for k in range(-3, last + 9):
+                j = k - 2
+                if 0 <= j < last:
+                    grouped_of[j] = work.tile([P, P, PACK], BF16, align_bytes=64, name="k_grouped")
+                    nc.scalar.activation(
+                        out=grouped_of[j][:], in_=half_of[j][:].rearrange("p t n -> p n t"), func=ACT.Exp, scale=-2.0
                     )
-                if p < NB:
-                    parts_of[p] = [zr] + max_terms(p)
-                    for d in range(3):
-                        parts_of[p].append(relu_term(p, d))
-                if p == 0:
+                j = k - 3
+                if 0 <= j < last:
+                    k_codes = work.tile([P, P], U32, align_bytes=64, name="k_codes")
+                    k_scales = work.tile([P, P], U8, align_bytes=64, name="k_scales")
+                    nc.vector.quantize_mx(
+                        out=k_codes[:].bitcast(FP8X4), scales=k_scales[:], in_=grouped_of[j][:].rearrange("p n t -> p (n t)")
+                    )
+                    codes_of[j] = (k_codes, k_scales)
+                b, second = divmod(k + 3, 2)
+                if b < NB:
+                    if second == 0:
+                        chains_of[b] = []
+                        relus_of[b] = []
+                        chain_step(b, chains_of[b], 0)
+                        chain_step(b, chains_of[b], 1)
+                        chain_step(b, chains_of[b], 2)
+                    else:
+                        chain_step(b, chains_of[b], 3)
+                        chain_step(b, chains_of[b], 4)
+                    for d in range(3 * second, 3 * second + 3):
+                        relus_of[b].append(relu_term(b, d))
+                if k == -2:
                     quantise_weights()
-                if 0 <= q < NB:
-                    early_half = sum_terms(parts_of[q], 0)
-                if 0 <= r:
-                    acc0 = multiply(k_codes, k_scales, 0)
-                if 0 <= q < NB:
-                    grouped_of[q] = work.tile([P, PASSES, P, PACK], BF16, align_bytes=64, name="k_grouped")
-                    exponential(grouped_of[q], early_half, 0)
-                if 0 <= r:
-                    result = work.tile([P, COLS], F32, name="result")
-                    nc.scalar.copy(out=result[:, 0:N_TILE], in_=acc0[:])
-                if p < NB:
-                    for d in range(3, N_RELU):
-                        parts_of[p].append(relu_term(p, d))
-                if 0 <= q < NB:
-                    late_half[q] = sum_terms(parts_of[q], 1)
-                if 0 <= r:
-                    acc1 = multiply(k_codes, k_scales, 1)
-                    nc.scalar.copy(out=result[:, N_TILE:COLS], in_=acc1[:])
-                    nc.sync.dma_start(out=out_blocks[r], in_=result[:])
+                if 0 <= k < last:
+                    half_of[k] = sum_terms([zr] + chains_of[k // 2] + relus_of[k // 2], k % 2)
+                j = k - 4
+                if 0 <= j < last:
+                    blk, c = divmod(j, 2)
+                    if c == 0:
+                        acc_of[blk] = [o_psum.tile([P, N_TILE], F32, name="acc") for h in range(COLS // N_TILE)]
+                    for h in range(COLS // N_TILE):
+                        nc.tensor.matmul_mx(
+                            out=acc_of[blk][h][:],
+                            lhsT=codes_of[j][0][:].bitcast(FP8X4),
+                            lhsT_scale=codes_of[j][1][:],
+                            rhs=w_codes[:, c, h * N_TILE : (h + 1) * N_TILE].bitcast(FP8X4),
+                            rhs_scale=w_scales[:, c, h * N_TILE : (h + 1) * N_TILE],
+                            start=(c == 0),
+                            stop=(c == PASSES - 1),
+                        )
+                blk, h = divmod(k - 7, 2)
+                if 0 <= blk < NB:
+                    if h == 0:
+                        result_of[blk] = work.tile([P, COLS], F32, name="result")
+                    nc.scalar.copy(out=result_of[blk][:, h * N_TILE : (h + 1) * N_TILE], in_=acc_of[blk][h][:])
+                    if h == 1:
+                        nc.sync.dma_start(out=out_blocks[blk], in_=result_of[blk][:])

@@ -24,7 +24,7 @@ LN_EPS = 1e-5
 FLOPS = 2 * N * M * COLS
 
 N_RELU = 6
-CHAINS = ((6, 8, 10, 12, 14), (7, 9, 11, 13, 15))
+CHAINS = ((6, 9, 12), (7, 10, 13), (8, 11, 14, 15))
 PLANE_ORDER = (0, 6, 1, 7, 2, 8, 3, 9, 4, 10, 5, 11, 12, 13, 14, 15)
 
 
@@ -142,7 +142,7 @@ def tile_tmk_kernel(tc, x, design_points, chol_inv, out):
                 lo = c * K_PASS + t * P
                 for i, part in enumerate(parts):
                     nc.tensor.matmul(
-                        out=half_l1[:, t, :], lhsT=part[:, lo : lo + P], rhs=ident[:], is_transpose=True,
+                        out=half_l1[:, t, :], lhsT=part[:, lo : lo + P], rhs=ident[:], is_transpose=(i > 0 or t == PACK - 1),
                         start=(i == 0), stop=(i == len(parts) - 1),
                     )
             return half_l1
@@ -178,10 +178,9 @@ def tile_tmk_kernel(tc, x, design_points, chol_inv, out):
                         relus_of[b] = []
                         chain_step(b, chains_of[b], 0)
                         chain_step(b, chains_of[b], 1)
-                        chain_step(b, chains_of[b], 2)
                     else:
+                        chain_step(b, chains_of[b], 2)
                         chain_step(b, chains_of[b], 3)
-                        chain_step(b, chains_of[b], 4)
                     for d in range(3 * second, 3 * second + 3):
                         relus_of[b].append(relu_term(b, d))
                 if k == -2:

@@ -24,7 +24,7 @@ LN_EPS = 1e-5
 FLOPS = 2 * N * M * COLS
 
 N_RELU = 6
-CHAINS = ((6, 9, 12), (7, 10, 13), (8, 11, 14, 15))
+CHAINS = ((6, 8, 10, 12, 14), (7, 9, 11, 13, 15))
 PLANE_ORDER = (0, 6, 1, 7, 2, 8, 3, 9, 4, 10, 5, 11, 12, 13, 14, 15)
 
 
@@ -142,7 +142,7 @@ def tile_tmk_kernel(tc, x, design_points, chol_inv, out):
                 lo = c * K_PASS + t * P
                 for i, part in enumerate(parts):
                     nc.tensor.matmul(
-                        out=half_l1[:, t, :], lhsT=part[:, lo : lo + P], rhs=ident[:], is_transpose=(i > 0 or t == PACK - 1),
+                        out=half_l1[:, t, :], lhsT=part[:, lo : lo + P], rhs=ident[:], is_transpose=True,
                         start=(i == 0), stop=(i == len(parts) - 1),
                     )
             return half_l1
@@ -155,7 +155,7 @@ def tile_tmk_kernel(tc, x, design_points, chol_inv, out):
         acc_of = {}
         result_of = {}
         last = PASSES * NB
-        with tc.manual_schedule():
+        if NB > 0:
             for k in range(-3, last + 9):
                 j = k - 2
                 if 0 <= j < last:
@@ -178,9 +178,10 @@ def tile_tmk_kernel(tc, x, design_points, chol_inv, out):
                         relus_of[b] = []
                         chain_step(b, chains_of[b], 0)
                         chain_step(b, chains_of[b], 1)
-                    else:
                         chain_step(b, chains_of[b], 2)
+                    else:
                         chain_step(b, chains_of[b], 3)
+                        chain_step(b, chains_of[b], 4)
                     for d in range(3 * second, 3 * second + 3):
                         relus_of[b].append(relu_term(b, d))
                 if k == -2:

@@ -90,10 +90,7 @@ def tile_tmk_kernel(tc, x, design_points, chol_inv, out):
                 for t in range(PACK):
                     lo = c * K_PASS + t * P
                     nc.tensor.transpose(plane[:, lo : lo + P], z_sb[:, c, t, d : d + 1].to_broadcast([P, P]), ident_bf[:])
-            if d < N_RELU:
-                nc.scalar.copy(out=zb[:, d, :], in_=plane[:])
-            else:
-                nc.vector.tensor_copy(out=zb[:, d, :], in_=plane[:])
+            nc.scalar.copy(out=zb[:, d, :], in_=plane[:])
         z_lo = setup.tile([P, PASSES, PACK], F32)
         nc.vector.tensor_reduce(out=z_lo[:], in_=z_sb[:, :, :, 0:N_RELU], axis=AX.X, op=ALU.add)
         z_hi = setup.tile([P, PASSES, PACK], F32)
@@ -105,11 +102,11 @@ def tile_tmk_kernel(tc, x, design_points, chol_inv, out):
             rest = q_psum.tile([P, PACK, P], F32, tag="q", name="rest")
             for t in range(PACK):
                 nc.tensor.transpose(rest[:, t, :], z_rest[:, c, t : t + 1].to_broadcast([P, P]), ident[:])
-            nc.vector.tensor_copy(out=zr[:, c * K_PASS : (c + 1) * K_PASS], in_=rest[:].rearrange("p t q -> p (t q)"))
+            nc.scalar.copy(out=zr[:, c * K_PASS : (c + 1) * K_PASS], in_=rest[:].rearrange("p t q -> p (t q)"))
 
         def quantise_weights():
             for c in range(PASSES):
-                w_grouped = setup.tile([P, COLS, PACK], BF16, tag="w_grouped", align_bytes=64)
+                w_grouped = setup.tile([P, COLS, PACK], BF16, name="w_grouped%d" % c, align_bytes=64)
                 nc.vector.tensor_copy(out=w_grouped[:], in_=w_raws[c][:].rearrange("p j w -> p w j"))
                 nc.vector.quantize_mx(
                     out=w_codes[:, c, :].bitcast(FP8X4),
@@ -146,6 +143,15 @@ def tile_tmk_kernel(tc, x, design_points, chol_inv, out):
                         start=(i == 0), stop=(i == len(parts) - 1),
                     )
             return half_l1
+
+        def fold_late_half(tiles):
+            while len(tiles) > 1:
+                for i in range(0, len(tiles), 2):
+                    nc.vector.tensor_tensor(
+                        out=tiles[i][:, K_PASS:M], in0=tiles[i][:, K_PASS:M], in1=tiles[i + 1][:, K_PASS:M], op=ALU.add
+                    )
+                tiles = tiles[0::2]
+            return tiles
 
         chains_of = {}
         relus_of = {}
@@ -186,8 +192,10 @@ def tile_tmk_kernel(tc, x, design_points, chol_inv, out):
                         relus_of[b].append(relu_term(b, d))
                 if k == -2:
                     quantise_weights()
-                if 0 <= k < last:
+                if 0 <= k < last - 1:
                     half_of[k] = sum_terms([zr] + chains_of[k // 2] + relus_of[k // 2], k % 2)
+                if k == last - 1:
+                    half_of[k] = sum_terms([zr] + fold_late_half(chains_of[k // 2] + relus_of[k // 2]), k % 2)
                 j = k - 4
                 if 0 <= j < last:
                     blk, c = divmod(j, 2)
@@ -207,6 +215,14 @@ def tile_tmk_kernel(tc, x, design_points, chol_inv, out):
                 if 0 <= blk < NB:
                     if h == 0:
                         result_of[blk] = work.tile([P, COLS], F32, name="result")
-                    nc.scalar.copy(out=result_of[blk][:, h * N_TILE : (h + 1) * N_TILE], in_=acc_of[blk][h][:])
-                    if h == 1:
-                        nc.sync.dma_start(out=out_blocks[blk], in_=result_of[blk][:])
+                    cols = slice(h * N_TILE, (h + 1) * N_TILE)
+                    if blk == NB - 1:
+                        if h == 0:
+                            nc.scalar.copy(out=result_of[blk][:, cols], in_=acc_of[blk][h][:])
+                        else:
+                            nc.vector.tensor_copy(out=result_of[blk][:, cols], in_=acc_of[blk][h][:])
+                        nc.sync.dma_start(out=out_blocks[blk][:, cols], in_=result_of[blk][:, cols])
+                    else:
+                        nc.scalar.copy(out=result_of[blk][:, cols], in_=acc_of[blk][h][:])
+                        if h == 1:
+                            nc.sync.dma_start(out=out_blocks[blk], in_=result_of[blk][:])

@@ -24,8 +24,9 @@ LN_EPS = 1e-5
 FLOPS = 2 * N * M * COLS
 
 N_RELU = 6
-CHAINS = ((6, 8, 10, 12, 14), (7, 9, 11, 13, 15))
-PLANE_ORDER = (0, 6, 1, 7, 2, 8, 3, 9, 4, 10, 5, 11, 12, 13, 14, 15)
+CHAINS = ((6, 10, 14), (7, 11, 15), (8, 12), (9, 13))
+FIRST_OPS = 6
+PLANE_ORDER = (6, 7, 0, 8, 9, 1, 10, 11, 2, 12, 13, 3, 14, 15, 4, 5)
 
 
 def tile_tmk_kernel(tc, x, design_points, chol_inv, out):
@@ -34,7 +35,7 @@ def tile_tmk_kernel(tc, x, design_points, chol_inv, out):
     with ExitStack() as stack:
         keep = stack.enter_context(tc.tile_pool(name="keep", bufs=1))
         setup = stack.enter_context(tc.tile_pool(name="setup", bufs=1))
-        terms = stack.enter_context(tc.tile_pool(name="terms", bufs=27))
+        terms = stack.enter_context(tc.tile_pool(name="terms", bufs=30))
         work = stack.enter_context(tc.tile_pool(name="work", bufs=4))
         q_psum = stack.enter_context(tc.psum_pool(name="q_psum", bufs=4))
         o_psum = stack.enter_context(tc.psum_pool(name="o_psum", bufs=4))
@@ -119,11 +120,9 @@ def tile_tmk_kernel(tc, x, design_points, chol_inv, out):
             nc.scalar.activation(out=part[:], in_=zb[:, d, :], func=ACT.Relu, bias=xn[:, b, d : d + 1], scale=-1.0)
             return part
 
-        def chain_step(b, chains, step):
-            for j, chain in enumerate(CHAINS):
-                if step >= len(chain):
-                    continue
-                d = chain[step]
+        def chain_ops(b, chains, ops):
+            for j, step in ops:
+                d = CHAINS[j][step]
                 if step == 0:
                     part = terms.tile([P, M], F32, tag="term", name="chain")
                     nc.vector.tensor_scalar(out=part[:], in0=zb[:, d, :], scalar1=xn[:, b, d : d + 1], scalar2=None, op0=ALU.max)
@@ -146,13 +145,14 @@ def tile_tmk_kernel(tc, x, design_points, chol_inv, out):
 
         def fold_late_half(tiles):
             while len(tiles) > 1:
-                for i in range(0, len(tiles), 2):
+                for i in range(0, len(tiles) - 1, 2):
                     nc.vector.tensor_tensor(
                         out=tiles[i][:, K_PASS:M], in0=tiles[i][:, K_PASS:M], in1=tiles[i + 1][:, K_PASS:M], op=ALU.add
                     )
                 tiles = tiles[0::2]
             return tiles
 
+        CHAIN_OPS = [(j, step) for step in range(3) for j in range(len(CHAINS)) if step < len(CHAINS[j])]
         chains_of = {}
         relus_of = {}
         half_of = {}
@@ -182,12 +182,9 @@ def tile_tmk_kernel(tc, x, design_points, chol_inv, out):
                     if second == 0:
                         chains_of[b] = []
                         relus_of[b] = []
-                        chain_step(b, chains_of[b], 0)
-                        chain_step(b, chains_of[b], 1)
-                        chain_step(b, chains_of[b], 2)
+                        chain_ops(b, chains_of[b], CHAIN_OPS[:FIRST_OPS])
                     else:
-                        chain_step(b, chains_of[b], 3)
-                        chain_step(b, chains_of[b], 4)
+                        chain_ops(b, chains_of[b], CHAIN_OPS[FIRST_OPS:])
                     for d in range(3 * second, 3 * second + 3):
                         relus_of[b].append(relu_term(b, d))
                 if k == -2:

@@ -24,7 +24,7 @@ LN_EPS = 1e-5
 FLOPS = 2 * N * M * COLS
 
 N_RELU = 6
-CHAINS = ((6, 10, 14), (7, 11, 15), (8, 12), (9, 13))
+CHAINS = ((6, 9, 12, 15), (7, 10, 13), (8, 11, 14))
 FIRST_OPS = 6
 PLANE_ORDER = (6, 7, 0, 8, 9, 1, 10, 11, 2, 12, 13, 3, 14, 15, 4, 5)
 
@@ -152,7 +152,7 @@ def tile_tmk_kernel(tc, x, design_points, chol_inv, out):
                 tiles = tiles[0::2]
             return tiles
 
-        CHAIN_OPS = [(j, step) for step in range(3) for j in range(len(CHAINS)) if step < len(CHAINS[j])]
+        CHAIN_OPS = [(j, step) for step in range(4) for j in range(len(CHAINS)) if step < len(CHAINS[j])]
         chains_of = {}
         relus_of = {}
         half_of = {}

@@ -24,7 +24,7 @@ LN_EPS = 1e-5
 FLOPS = 2 * N * M * COLS
 
 N_RELU = 6
-CHAINS = ((6, 9, 12, 15), (7, 10, 13), (8, 11, 14))
+CHAIN_SETS = (((6, 8, 10, 12, 14), (7, 9, 11, 13, 15)), ((6, 9, 12, 15), (7, 10, 13), (8, 11, 14)))
 FIRST_OPS = 6
 PLANE_ORDER = (6, 7, 0, 8, 9, 1, 10, 11, 2, 12, 13, 3, 14, 15, 4, 5)
 
@@ -120,9 +120,11 @@ def tile_tmk_kernel(tc, x, design_points, chol_inv, out):
             nc.scalar.activation(out=part[:], in_=zb[:, d, :], func=ACT.Relu, bias=xn[:, b, d : d + 1], scale=-1.0)
             return part
 
-        def chain_ops(b, chains, ops):
-            for j, step in ops:
-                d = CHAINS[j][step]
+        def chain_ops(b, chains, first):
+            chain_set = CHAIN_SETS[b % len(CHAIN_SETS)]
+            ops = [(j, step) for step in range(D) for j in range(len(chain_set)) if step < len(chain_set[j])]
+            for j, step in ops[:FIRST_OPS] if first else ops[FIRST_OPS:]:
+                d = chain_set[j][step]
                 if step == 0:
                     part = terms.tile([P, M], F32, tag="term", name="chain")
                     nc.vector.tensor_scalar(out=part[:], in0=zb[:, d, :], scalar1=xn[:, b, d : d + 1], scalar2=None, op0=ALU.max)
@@ -152,7 +154,6 @@ def tile_tmk_kernel(tc, x, design_points, chol_inv, out):
                 tiles = tiles[0::2]
             return tiles
 
-        CHAIN_OPS = [(j, step) for step in range(4) for j in range(len(CHAINS)) if step < len(CHAINS[j])]
         chains_of = {}
         relus_of = {}
         half_of = {}
@@ -182,9 +183,9 @@ def tile_tmk_kernel(tc, x, design_points, chol_inv, out):
                     if second == 0:
                         chains_of[b] = []
                         relus_of[b] = []
-                        chain_ops(b, chains_of[b], CHAIN_OPS[:FIRST_OPS])
+                        chain_ops(b, chains_of[b], True)
                     else:
-                        chain_ops(b, chains_of[b], CHAIN_OPS[FIRST_OPS:])
+                        chain_ops(b, chains_of[b], False)
                     for d in range(3 * second, 3 * second + 3):
                         relus_of[b].append(relu_term(b, d))
                 if k == -2:

@@ -23,9 +23,10 @@ N_TILE = 512
 LN_EPS = 1e-5
 FLOPS = 2 * N * M * COLS
 
-N_RELU = 6
-CHAIN_SETS = (((6, 8, 10, 12, 14), (7, 9, 11, 13, 15)), ((6, 9, 12, 15), (7, 10, 13), (8, 11, 14)))
-FIRST_OPS = 6
+TWO_CHAINS = (6, ((6, 8, 10, 12, 14), (7, 9, 11, 13, 15)))
+THREE_CHAINS = (6, ((6, 9, 12, 15), (7, 10, 13), (8, 11, 14)))
+SEVEN_RELUS = (7, ((7, 9, 11, 13, 15), (8, 10, 12, 14)))
+RECIPES = (TWO_CHAINS, THREE_CHAINS, TWO_CHAINS, SEVEN_RELUS)
 PLANE_ORDER = (6, 7, 0, 8, 9, 1, 10, 11, 2, 12, 13, 3, 14, 15, 4, 5)
 
 
@@ -35,7 +36,7 @@ def tile_tmk_kernel(tc, x, design_points, chol_inv, out):
     with ExitStack() as stack:
         keep = stack.enter_context(tc.tile_pool(name="keep", bufs=1))
         setup = stack.enter_context(tc.tile_pool(name="setup", bufs=1))
-        terms = stack.enter_context(tc.tile_pool(name="terms", bufs=30))
+        terms = stack.enter_context(tc.tile_pool(name="terms", bufs=29))
         work = stack.enter_context(tc.tile_pool(name="work", bufs=4))
         q_psum = stack.enter_context(tc.psum_pool(name="q_psum", bufs=4))
         o_psum = stack.enter_context(tc.psum_pool(name="o_psum", bufs=4))
@@ -57,7 +58,7 @@ def tile_tmk_kernel(tc, x, design_points, chol_inv, out):
         ident_bf = keep.tile([P, P], BF16)
         make_identity(nc, ident_bf[:])
         zb = keep.tile([P, D, M], BF16)
-        zr = keep.tile([P, M], F32)
+        zr_of = {}
         w_codes = keep.tile([P, PASSES, COLS], U32, align_bytes=64)
         w_scales = keep.tile([P, PASSES, COLS], U8, align_bytes=64)
         xn = keep.tile([P, NB, D], F32)
@@ -92,18 +93,20 @@ def tile_tmk_kernel(tc, x, design_points, chol_inv, out):
                     lo = c * K_PASS + t * P
                     nc.tensor.transpose(plane[:, lo : lo + P], z_sb[:, c, t, d : d + 1].to_broadcast([P, P]), ident_bf[:])
             nc.scalar.copy(out=zb[:, d, :], in_=plane[:])
-        z_lo = setup.tile([P, PASSES, PACK], F32)
-        nc.vector.tensor_reduce(out=z_lo[:], in_=z_sb[:, :, :, 0:N_RELU], axis=AX.X, op=ALU.add)
-        z_hi = setup.tile([P, PASSES, PACK], F32)
-        nc.vector.tensor_reduce(out=z_hi[:], in_=z_sb[:, :, :, N_RELU:D], axis=AX.X, op=ALU.add)
-        z_rest = setup.tile([P, PASSES, PACK], F32)
-        nc.vector.tensor_tensor(out=z_rest[:], in0=z_lo[:], in1=z_hi[:], op=ALU.subtract)
-        nc.vector.tensor_scalar_mul(out=z_rest[:], in0=z_rest[:], scalar1=0.5)
-        for c in range(PASSES):
-            rest = q_psum.tile([P, PACK, P], F32, tag="q", name="rest")
-            for t in range(PACK):
-                nc.tensor.transpose(rest[:, t, :], z_rest[:, c, t : t + 1].to_broadcast([P, P]), ident[:])
-            nc.scalar.copy(out=zr[:, c * K_PASS : (c + 1) * K_PASS], in_=rest[:].rearrange("p t q -> p (t q)"))
+        for a in sorted(set(recipe[0] for recipe in RECIPES)):
+            zr_of[a] = keep.tile([P, M], F32, name="zr%d" % a)
+            z_lo = setup.tile([P, PASSES, PACK], F32, name="z_lo%d" % a)
+            nc.vector.tensor_reduce(out=z_lo[:], in_=z_sb[:, :, :, 0:a], axis=AX.X, op=ALU.add)
+            z_hi = setup.tile([P, PASSES, PACK], F32, name="z_hi%d" % a)
+            nc.vector.tensor_reduce(out=z_hi[:], in_=z_sb[:, :, :, a:D], axis=AX.X, op=ALU.add)
+            z_rest = setup.tile([P, PASSES, PACK], F32, name="z_rest%d" % a)
+            nc.vector.tensor_tensor(out=z_rest[:], in0=z_lo[:], in1=z_hi[:], op=ALU.subtract)
+            nc.vector.tensor_scalar_mul(out=z_rest[:], in0=z_rest[:], scalar1=0.5)
+            for c in range(PASSES):
+                rest = q_psum.tile([P, PACK, P], F32, tag="q", name="rest")
+                for t in range(PACK):
+                    nc.tensor.transpose(rest[:, t, :], z_rest[:, c, t : t + 1].to_broadcast([P, P]), ident[:])
+                nc.scalar.copy(out=zr_of[a][:, c * K_PASS : (c + 1) * K_PASS], in_=rest[:].rearrange("p t q -> p (t q)"))
 
         def quantise_weights():
             for c in range(PASSES):
@@ -121,10 +124,11 @@ def tile_tmk_kernel(tc, x, design_points, chol_inv, out):
             return part
 
         def chain_ops(b, chains, first):
-            chain_set = CHAIN_SETS[b % len(CHAIN_SETS)]
-            ops = [(j, step) for step in range(D) for j in range(len(chain_set)) if step < len(chain_set[j])]
-            for j, step in ops[:FIRST_OPS] if first else ops[FIRST_OPS:]:
-                d = chain_set[j][step]
+            own = RECIPES[b % len(RECIPES)][1]
+            ops = [(j, step) for step in range(D) for j in range(len(own)) if step < len(own[j])]
+            n_first = (len(ops) + 2) // 2
+            for j, step in ops[:n_first] if first else ops[n_first:]:
+                d = own[j][step]
                 if step == 0:
                     part = terms.tile([P, M], F32, tag="term", name="chain")
                     nc.vector.tensor_scalar(out=part[:], in0=zb[:, d, :], scalar1=xn[:, b, d : d + 1], scalar2=None, op0=ALU.max)
@@ -180,20 +184,21 @@ def tile_tmk_kernel(tc, x, design_points, chol_inv, out):
                     codes_of[j] = (k_codes, k_scales)
                 b, second = divmod(k + 3, 2)
                 if b < NB:
+                    n_relu = RECIPES[b % len(RECIPES)][0]
                     if second == 0:
                         chains_of[b] = []
                         relus_of[b] = []
-                        chain_ops(b, chains_of[b], True)
-                    else:
-                        chain_ops(b, chains_of[b], False)
-                    for d in range(3 * second, 3 * second + 3):
+                    chain_ops(b, chains_of[b], second == 0)
+                    for d in range((n_relu + 1) // 2) if second == 0 else range((n_relu + 1) // 2, n_relu):
                         relus_of[b].append(relu_term(b, d))
                 if k == -2:
                     quantise_weights()
                 if 0 <= k < last - 1:
-                    half_of[k] = sum_terms([zr] + chains_of[k // 2] + relus_of[k // 2], k % 2)
+                    half_of[k] = sum_terms([zr_of[RECIPES[k // 2 % len(RECIPES)][0]]] + chains_of[k // 2] + relus_of[k // 2], k % 2)
                 if k == last - 1:
-                    half_of[k] = sum_terms([zr] + fold_late_half(chains_of[k // 2] + relus_of[k // 2]), k % 2)
+                    half_of[k] = sum_terms(
+                        [zr_of[RECIPES[k // 2 % len(RECIPES)][0]]] + fold_late_half(chains_of[k // 2] + relus_of[k // 2]), k % 2
+                    )
                 j = k - 4
                 if 0 <= j < last:
                     blk, c = divmod(j, 2)

@@ -24,9 +24,8 @@ LN_EPS = 1e-5
 FLOPS = 2 * N * M * COLS
 
 TWO_CHAINS = (6, ((6, 8, 10, 12, 14), (7, 9, 11, 13, 15)))
-THREE_CHAINS = (6, ((6, 9, 12, 15), (7, 10, 13), (8, 11, 14)))
 SEVEN_RELUS = (7, ((7, 9, 11, 13, 15), (8, 10, 12, 14)))
-RECIPES = (TWO_CHAINS, THREE_CHAINS, TWO_CHAINS, SEVEN_RELUS)
+RECIPES = (TWO_CHAINS, SEVEN_RELUS)
 PLANE_ORDER = (6, 7, 0, 8, 9, 1, 10, 11, 2, 12, 13, 3, 14, 15, 4, 5)
 
 

@@ -23,10 +23,12 @@ N_TILE = 512
 LN_EPS = 1e-5
 FLOPS = 2 * N * M * COLS
 
-TWO_CHAINS = (6, ((6, 8, 10, 12, 14), (7, 9, 11, 13, 15)))
-SEVEN_RELUS = (7, ((7, 9, 11, 13, 15), (8, 10, 12, 14)))
-RECIPES = (TWO_CHAINS, SEVEN_RELUS)
+TWO_CHAINS = (6, ((6, 8, 10, 12, 14), (7, 9, 11, 13, 15)), False)
+SEVEN_RELUS = (7, ((7, 9, 11, 13, 15), (8, 10, 12, 14)), False)
+SEVEN_RELUS_ZR = (7, ((7, 9, 11, 13, 15), (8, 10, 12, 14)), True)
+RECIPES = (TWO_CHAINS, SEVEN_RELUS, TWO_CHAINS, SEVEN_RELUS)
 PLANE_ORDER = (6, 7, 0, 8, 9, 1, 10, 11, 2, 12, 13, 3, 14, 15, 4, 5)
+EARLY_PLANES = 3
 
 
 def tile_tmk_kernel(tc, x, design_points, chol_inv, out):
@@ -74,24 +76,29 @@ def tile_tmk_kernel(tc, x, design_points, chol_inv, out):
         var = setup.tile([P, NB], F32)
         nc.vector.tensor_reduce(out=var[:], in_=sq[:], axis=AX.X, op=ALU.add)
         nc.vector.tensor_scalar(out=var[:], in0=var[:], scalar1=1.0 / D, scalar2=LN_EPS, op0=ALU.mult, op1=ALU.add)
-        std = setup.tile([P, NB], F32)
-        nc.scalar.activation(out=std[:], in_=var[:], func=ACT.Sqrt)
-        rstd = setup.tile([P, NB], F32)
-        nc.vector.reciprocal(out=rstd[:], in_=std[:])
-        nt = setup.tile([P, NB], F32)
-        nc.vector.tensor_tensor(out=nt[:], in0=rstd[:], in1=rstd[:], op=ALU.mult)
-        nc.vector.tensor_tensor(out=nt[:], in0=nt[:], in1=var[:], op=ALU.mult)
-        nc.vector.tensor_scalar(out=nt[:], in0=nt[:], scalar1=-0.5, scalar2=1.5, op0=ALU.mult, op1=ALU.add)
-        nc.vector.tensor_tensor(out=rstd[:], in0=rstd[:], in1=nt[:], op=ALU.mult)
-        nc.vector.tensor_tensor(out=xn[:], in0=xc[:], in1=rstd[:].unsqueeze(2).to_broadcast([P, NB, D]), op=ALU.mult)
+        def spread_planes(coordinates):
+            for d in coordinates:
+                plane = q_psum.tile([P, M], BF16, tag="q", name="plane")
+                for c in range(PASSES):
+                    for t in range(PACK):
+                        lo = c * K_PASS + t * P
+                        nc.tensor.transpose(plane[:, lo : lo + P], z_sb[:, c, t, d : d + 1].to_broadcast([P, P]), ident_bf[:])
+                nc.scalar.copy(out=zb[:, d, :], in_=plane[:])
 
-        for d in PLANE_ORDER:
-            plane = q_psum.tile([P, M], BF16, tag="q", name="plane")
-            for c in range(PASSES):
-                for t in range(PACK):
-                    lo = c * K_PASS + t * P
-                    nc.tensor.transpose(plane[:, lo : lo + P], z_sb[:, c, t, d : d + 1].to_broadcast([P, P]), ident_bf[:])
-            nc.scalar.copy(out=zb[:, d, :], in_=plane[:])
+        with tc.manual_schedule(engines={mybir.EngineType.Activation}):
+            spread_planes(PLANE_ORDER[:EARLY_PLANES])
+            std = setup.tile([P, NB], F32)
+            nc.scalar.activation(out=std[:], in_=var[:], func=ACT.Sqrt)
+            rstd = setup.tile([P, NB], F32)
+            nc.vector.reciprocal(out=rstd[:], in_=std[:])
+            nt = setup.tile([P, NB], F32)
+            nc.vector.tensor_tensor(out=nt[:], in0=rstd[:], in1=rstd[:], op=ALU.mult)
+            nc.vector.tensor_tensor(out=nt[:], in0=nt[:], in1=var[:], op=ALU.mult)
+            nc.vector.tensor_scalar(out=nt[:], in0=nt[:], scalar1=-0.5, scalar2=1.5, op0=ALU.mult, op1=ALU.add)
+            nc.vector.tensor_tensor(out=rstd[:], in0=rstd[:], in1=nt[:], op=ALU.mult)
+            nc.vector.tensor_tensor(out=xn[:], in0=xc[:], in1=rstd[:].unsqueeze(2).to_broadcast([P, NB, D]), op=ALU.mult)
+
+            spread_planes(PLANE_ORDER[EARLY_PLANES:])
         for a in sorted(set(recipe[0] for recipe in RECIPES)):
             zr_of[a] = keep.tile([P, M], F32, name="zr%d" % a)
             z_lo = setup.tile([P, PASSES, PACK], F32, name="z_lo%d" % a)
@@ -123,19 +130,30 @@ def tile_tmk_kernel(tc, x, design_points, chol_inv, out):
             return part
 
         def chain_ops(b, chains, first):
-            own = RECIPES[b % len(RECIPES)][1]
+            a, own, zr_on_vector = RECIPES[b % len(RECIPES)]
             ops = [(j, step) for step in range(D) for j in range(len(own)) if step < len(own[j])]
             n_first = (len(ops) + 2) // 2
             for j, step in ops[:n_first] if first else ops[n_first:]:
                 d = own[j][step]
                 if step == 0:
                     part = terms.tile([P, M], F32, tag="term", name="chain")
-                    nc.vector.tensor_scalar(out=part[:], in0=zb[:, d, :], scalar1=xn[:, b, d : d + 1], scalar2=None, op0=ALU.max)
+                    if zr_on_vector and j == len(own) - 1:
+                        nc.vector.scalar_tensor_tensor(
+                            out=part[:], in0=zb[:, d, :], scalar=xn[:, b, d : d + 1], in1=zr_of[a][:], op0=ALU.max, op1=ALU.add
+                        )
+                    else:
+                        nc.vector.tensor_scalar(
+                            out=part[:], in0=zb[:, d, :], scalar1=xn[:, b, d : d + 1], scalar2=None, op0=ALU.max
+                        )
                     chains.append(part)
                 else:
                     nc.vector.scalar_tensor_tensor(
                         out=chains[j][:], in0=zb[:, d, :], scalar=xn[:, b, d : d + 1], in1=chains[j][:], op0=ALU.max, op1=ALU.add
                     )
+
+        def zr_part(b):
+            a, own, zr_on_vector = RECIPES[b % len(RECIPES)]
+            return [] if zr_on_vector else [zr_of[a]]
 
         def sum_terms(parts, c):
             half_l1 = q_psum.tile([P, PACK, P], F32, tag="q", name="half_l1")
@@ -193,11 +211,9 @@ def tile_tmk_kernel(tc, x, design_points, chol_inv, out):
                 if k == -2:
                     quantise_weights()
                 if 0 <= k < last - 1:
-                    half_of[k] = sum_terms([zr_of[RECIPES[k // 2 % len(RECIPES)][0]]] + chains_of[k // 2] + relus_of[k // 2], k % 2)
+                    half_of[k] = sum_terms(zr_part(k // 2) + chains_of[k // 2] + relus_of[k // 2], k % 2)
                 if k == last - 1:
-                    half_of[k] = sum_terms(
-                        [zr_of[RECIPES[k // 2 % len(RECIPES)][0]]] + fold_late_half(chains_of[k // 2] + relus_of[k // 2]), k % 2
-                    )
+                    half_of[k] = sum_terms(zr_part(k // 2) + fold_late_half(chains_of[k // 2] + relus_of[k // 2]), k % 2)
                 j = k - 4
                 if 0 <= j < last:
                     blk, c = divmod(j, 2)

@@ -23,10 +23,10 @@ N_TILE = 512
 LN_EPS = 1e-5
 FLOPS = 2 * N * M * COLS
 
-TWO_CHAINS = (6, ((6, 8, 10, 12, 14), (7, 9, 11, 13, 15)), False)
-SEVEN_RELUS = (7, ((7, 9, 11, 13, 15), (8, 10, 12, 14)), False)
-SEVEN_RELUS_ZR = (7, ((7, 9, 11, 13, 15), (8, 10, 12, 14)), True)
-RECIPES = (TWO_CHAINS, SEVEN_RELUS, TWO_CHAINS, SEVEN_RELUS)
+RELUS = (0, 1, 2, 3, 4, 5)
+CHAINS = ((6, 8, 10, 12, 14), (7, 9, 11, 13, 15))
+IN_PSUM = (8, 9, 10, 11)
+BIG = 3.4028234663852886e38
 PLANE_ORDER = (6, 7, 0, 8, 9, 1, 10, 11, 2, 12, 13, 3, 14, 15, 4, 5)
 EARLY_PLANES = 3
 
@@ -37,10 +37,12 @@ def tile_tmk_kernel(tc, x, design_points, chol_inv, out):
     with ExitStack() as stack:
         keep = stack.enter_context(tc.tile_pool(name="keep", bufs=1))
         setup = stack.enter_context(tc.tile_pool(name="setup", bufs=1))
-        terms = stack.enter_context(tc.tile_pool(name="terms", bufs=29))
+        terms = stack.enter_context(tc.tile_pool(name="terms", bufs=27))
         work = stack.enter_context(tc.tile_pool(name="work", bufs=4))
-        q_psum = stack.enter_context(tc.psum_pool(name="q_psum", bufs=4))
-        o_psum = stack.enter_context(tc.psum_pool(name="o_psum", bufs=4))
+        seeds = stack.enter_context(tc.tile_pool(name="seeds", bufs=1))
+        q_psum = stack.enter_context(tc.psum_pool(name="q_psum", bufs=3))
+        o_psum = stack.enter_context(tc.psum_pool(name="o_psum", bufs=1))
+        z_psum = stack.enter_context(tc.psum_pool(name="z_psum", bufs=1))
 
         x_raw = setup.tile([P, NB, D], BF16)
         nc.sync.dma_start(out=x_raw[:], in_=x.rearrange("(p b) d -> p b d", b=NB))
@@ -59,7 +61,8 @@ def tile_tmk_kernel(tc, x, design_points, chol_inv, out):
         ident_bf = keep.tile([P, P], BF16)
         make_identity(nc, ident_bf[:])
         zb = keep.tile([P, D, M], BF16)
-        zr_of = {}
+        z_plane = {}
+        zr = keep.tile([P, M], F32)
         w_codes = keep.tile([P, PASSES, COLS], U32, align_bytes=64)
         w_scales = keep.tile([P, PASSES, COLS], U8, align_bytes=64)
         xn = keep.tile([P, NB, D], F32)
@@ -78,12 +81,19 @@ def tile_tmk_kernel(tc, x, design_points, chol_inv, out):
         nc.vector.tensor_scalar(out=var[:], in0=var[:], scalar1=1.0 / D, scalar2=LN_EPS, op0=ALU.mult, op1=ALU.add)
         def spread_planes(coordinates):
             for d in coordinates:
-                plane = q_psum.tile([P, M], BF16, tag="q", name="plane")
+                if d in IN_PSUM:
+                    plane = z_psum.tile([P, M], BF16, name="plane%d" % d)
+                else:
+                    plane = q_psum.tile([P, M], BF16, tag="q", name="plane")
                 for c in range(PASSES):
                     for t in range(PACK):
                         lo = c * K_PASS + t * P
                         nc.tensor.transpose(plane[:, lo : lo + P], z_sb[:, c, t, d : d + 1].to_broadcast([P, P]), ident_bf[:])
-                nc.scalar.copy(out=zb[:, d, :], in_=plane[:])
+                if d in IN_PSUM:
+                    z_plane[d] = plane[:]
+                else:
+                    nc.scalar.copy(out=zb[:, d, :], in_=plane[:])
+                    z_plane[d] = zb[:, d, :]
 
         with tc.manual_schedule(engines={mybir.EngineType.Activation}):
             spread_planes(PLANE_ORDER[:EARLY_PLANES])
@@ -99,20 +109,19 @@ def tile_tmk_kernel(tc, x, design_points, chol_inv, out):
             nc.vector.tensor_tensor(out=xn[:], in0=xc[:], in1=rstd[:].unsqueeze(2).to_broadcast([P, NB, D]), op=ALU.mult)
 
             spread_planes(PLANE_ORDER[EARLY_PLANES:])
-        for a in sorted(set(recipe[0] for recipe in RECIPES)):
-            zr_of[a] = keep.tile([P, M], F32, name="zr%d" % a)
-            z_lo = setup.tile([P, PASSES, PACK], F32, name="z_lo%d" % a)
-            nc.vector.tensor_reduce(out=z_lo[:], in_=z_sb[:, :, :, 0:a], axis=AX.X, op=ALU.add)
-            z_hi = setup.tile([P, PASSES, PACK], F32, name="z_hi%d" % a)
-            nc.vector.tensor_reduce(out=z_hi[:], in_=z_sb[:, :, :, a:D], axis=AX.X, op=ALU.add)
-            z_rest = setup.tile([P, PASSES, PACK], F32, name="z_rest%d" % a)
-            nc.vector.tensor_tensor(out=z_rest[:], in0=z_lo[:], in1=z_hi[:], op=ALU.subtract)
-            nc.vector.tensor_scalar_mul(out=z_rest[:], in0=z_rest[:], scalar1=0.5)
-            for c in range(PASSES):
-                rest = q_psum.tile([P, PACK, P], F32, tag="q", name="rest")
-                for t in range(PACK):
-                    nc.tensor.transpose(rest[:, t, :], z_rest[:, c, t : t + 1].to_broadcast([P, P]), ident[:])
-                nc.scalar.copy(out=zr_of[a][:, c * K_PASS : (c + 1) * K_PASS], in_=rest[:].rearrange("p t q -> p (t q)"))
+        n_relu = len(RELUS)
+        z_lo = setup.tile([P, PASSES, PACK], F32)
+        nc.vector.tensor_reduce(out=z_lo[:], in_=z_sb[:, :, :, 0:n_relu], axis=AX.X, op=ALU.add)
+        z_hi = setup.tile([P, PASSES, PACK], F32)
+        nc.vector.tensor_reduce(out=z_hi[:], in_=z_sb[:, :, :, n_relu:D], axis=AX.X, op=ALU.add)
+        z_rest = setup.tile([P, PASSES, PACK], F32)
+        nc.vector.tensor_tensor(out=z_rest[:], in0=z_lo[:], in1=z_hi[:], op=ALU.subtract)
+        nc.vector.tensor_scalar_mul(out=z_rest[:], in0=z_rest[:], scalar1=0.5)
+        for c in range(PASSES):
+            rest = q_psum.tile([P, PACK, P], F32, tag="q", name="rest")
+            for t in range(PACK):
+                nc.tensor.transpose(rest[:, t, :], z_rest[:, c, t : t + 1].to_broadcast([P, P]), ident[:])
+            nc.scalar.copy(out=zr[:, c * K_PASS : (c + 1) * K_PASS], in_=rest[:].rearrange("p t q -> p (t q)"))
 
         def quantise_weights():
             for c in range(PASSES):
@@ -129,31 +138,30 @@ def tile_tmk_kernel(tc, x, design_points, chol_inv, out):
             nc.scalar.activation(out=part[:], in_=zb[:, d, :], func=ACT.Relu, bias=xn[:, b, d : d + 1], scale=-1.0)
             return part
 
-        def chain_ops(b, chains, first):
-            a, own, zr_on_vector = RECIPES[b % len(RECIPES)]
-            ops = [(j, step) for step in range(D) for j in range(len(own)) if step < len(own[j])]
-            n_first = (len(ops) + 2) // 2
-            for j, step in ops[:n_first] if first else ops[n_first:]:
-                d = own[j][step]
-                if step == 0:
-                    part = terms.tile([P, M], F32, tag="term", name="chain")
-                    if zr_on_vector and j == len(own) - 1:
-                        nc.vector.scalar_tensor_tensor(
-                            out=part[:], in0=zb[:, d, :], scalar=xn[:, b, d : d + 1], in1=zr_of[a][:], op0=ALU.max, op1=ALU.add
-                        )
-                    else:
-                        nc.vector.tensor_scalar(
-                            out=part[:], in0=zb[:, d, :], scalar1=xn[:, b, d : d + 1], scalar2=None, op0=ALU.max
-                        )
-                    chains.append(part)
+        def make_seeds(b):
+            made = []
+            for j, chain in enumerate(CHAINS):
+                d = chain[0]
+                seed = seeds.tile([P, M], F32, name="seed%d" % j)
+                x_col = xn[:, b, d : d + 1]
+                if b == 0:
+                    nc.vector.tensor_scalar(out=seed[:], in0=z_plane[d], scalar1=x_col, scalar2=None, op0=ALU.max)
                 else:
-                    nc.vector.scalar_tensor_tensor(
-                        out=chains[j][:], in0=zb[:, d, :], scalar=xn[:, b, d : d + 1], in1=chains[j][:], op0=ALU.max, op1=ALU.add
-                    )
+                    nc.gpsimd.tensor_scalar(out=seed[:], in0=z_plane[d], scalar1=BIG, scalar2=x_col, op0=ALU.min, op1=ALU.max)
+                made.append(seed)
+            return made
 
-        def zr_part(b):
-            a, own, zr_on_vector = RECIPES[b % len(RECIPES)]
-            return [] if zr_on_vector else [zr_of[a]]
+        def chain_ops(b, chains, first):
+            ops = [(j, step) for step in range(1, len(CHAINS[0])) for j in range(len(CHAINS))]
+            half = len(ops) // 2
+            for j, step in ops[:half] if first else ops[half:]:
+                d = CHAINS[j][step]
+                if step == 1:
+                    chains.append(terms.tile([P, M], F32, tag="term", name="chain"))
+                before = seeds_of[b][j] if step == 1 else chains[j]
+                nc.vector.scalar_tensor_tensor(
+                    out=chains[j][:], in0=z_plane[d], scalar=xn[:, b, d : d + 1], in1=before[:], op0=ALU.max, op1=ALU.add
+                )
 
         def sum_terms(parts, c):
             half_l1 = q_psum.tile([P, PACK, P], F32, tag="q", name="half_l1")
@@ -175,6 +183,7 @@ def tile_tmk_kernel(tc, x, design_points, chol_inv, out):
                 tiles = tiles[0::2]
             return tiles
 
+        seeds_of = {0: make_seeds(0)}
         chains_of = {}
         relus_of = {}
         half_of = {}
@@ -183,64 +192,65 @@ def tile_tmk_kernel(tc, x, design_points, chol_inv, out):
         acc_of = {}
         result_of = {}
         last = PASSES * NB
-        if NB > 0:
-            for k in range(-3, last + 9):
-                j = k - 2
-                if 0 <= j < last:
-                    grouped_of[j] = work.tile([P, P, PACK], BF16, align_bytes=64, name="k_grouped")
-                    nc.scalar.activation(
-                        out=grouped_of[j][:], in_=half_of[j][:].rearrange("p t n -> p n t"), func=ACT.Exp, scale=-2.0
-                    )
-                j = k - 3
-                if 0 <= j < last:
-                    k_codes = work.tile([P, P], U32, align_bytes=64, name="k_codes")
-                    k_scales = work.tile([P, P], U8, align_bytes=64, name="k_scales")
-                    nc.vector.quantize_mx(
-                        out=k_codes[:].bitcast(FP8X4), scales=k_scales[:], in_=grouped_of[j][:].rearrange("p n t -> p (n t)")
-                    )
-                    codes_of[j] = (k_codes, k_scales)
-                b, second = divmod(k + 3, 2)
-                if b < NB:
-                    n_relu = RECIPES[b % len(RECIPES)][0]
-                    if second == 0:
-                        chains_of[b] = []
-                        relus_of[b] = []
-                    chain_ops(b, chains_of[b], second == 0)
-                    for d in range((n_relu + 1) // 2) if second == 0 else range((n_relu + 1) // 2, n_relu):
-                        relus_of[b].append(relu_term(b, d))
-                if k == -2:
-                    quantise_weights()
-                if 0 <= k < last - 1:
-                    half_of[k] = sum_terms(zr_part(k // 2) + chains_of[k // 2] + relus_of[k // 2], k % 2)
-                if k == last - 1:
-                    half_of[k] = sum_terms(zr_part(k // 2) + fold_late_half(chains_of[k // 2] + relus_of[k // 2]), k % 2)
-                j = k - 4
-                if 0 <= j < last:
-                    blk, c = divmod(j, 2)
-                    if c == 0:
-                        acc_of[blk] = [o_psum.tile([P, N_TILE], F32, name="acc") for h in range(COLS // N_TILE)]
-                    for h in range(COLS // N_TILE):
-                        nc.tensor.matmul_mx(
-                            out=acc_of[blk][h][:],
-                            lhsT=codes_of[j][0][:].bitcast(FP8X4),
-                            lhsT_scale=codes_of[j][1][:],
-                            rhs=w_codes[:, c, h * N_TILE : (h + 1) * N_TILE].bitcast(FP8X4),
-                            rhs_scale=w_scales[:, c, h * N_TILE : (h + 1) * N_TILE],
-                            start=(c == 0),
-                            stop=(c == PASSES - 1),
-                        )
-                blk, h = divmod(k - 7, 2)
-                if 0 <= blk < NB:
+        for k in range(-3, last + 9):
+            j = k - 2
+            if 0 <= j < last:
+                grouped_of[j] = work.tile([P, P, PACK], BF16, align_bytes=64, name="k_grouped")
+                nc.scalar.activation(
+                    out=grouped_of[j][:], in_=half_of[j][:].rearrange("p t n -> p n t"), func=ACT.Exp, scale=-2.0
+                )
+            j = k - 3
+            if 0 <= j < last:
+                k_codes = work.tile([P, P], U32, align_bytes=64, name="k_codes")
+                k_scales = work.tile([P, P], U8, align_bytes=64, name="k_scales")
+                nc.vector.quantize_mx(
+                    out=k_codes[:].bitcast(FP8X4), scales=k_scales[:], in_=grouped_of[j][:].rearrange("p n t -> p (n t)")
+                )
+                codes_of[j] = (k_codes, k_scales)
+            b, second = divmod(k + 3, 2)
+            if b < NB:
+                if second == 0:
+                    chains_of[b] = []
+                    relus_of[b] = []
+                chain_ops(b, chains_of[b], second == 0)
+                if second == 0 and b + 1 < NB:
+                    seeds_of[b + 1] = make_seeds(b + 1)
+                for d in RELUS[: n_relu // 2] if second == 0 else RELUS[n_relu // 2 :]:
+                    relus_of[b].append(relu_term(b, d))
+            if k == -2:
+                quantise_weights()
+            if 0 <= k < last - 1:
+                half_of[k] = sum_terms([zr] + chains_of[k // 2] + relus_of[k // 2], k % 2)
+            if k == last - 1:
+                half_of[k] = sum_terms([zr] + fold_late_half(chains_of[k // 2] + relus_of[k // 2]), k % 2)
+            blk, h = divmod(k - 6, 2)
+            if 0 <= blk < NB:
+                if h == 0:
+                    result_of[blk] = work.tile([P, COLS], F32, name="result")
+                cols = slice(h * N_TILE, (h + 1) * N_TILE)
+                if blk == NB - 1:
                     if h == 0:
-                        result_of[blk] = work.tile([P, COLS], F32, name="result")
-                    cols = slice(h * N_TILE, (h + 1) * N_TILE)
-                    if blk == NB - 1:
-                        if h == 0:
-                            nc.scalar.copy(out=result_of[blk][:, cols], in_=acc_of[blk][h][:])
-                        else:
-                            nc.vector.tensor_copy(out=result_of[blk][:, cols], in_=acc_of[blk][h][:])
-                        nc.sync.dma_start(out=out_blocks[blk][:, cols], in_=result_of[blk][:, cols])
+                        nc.scalar.copy(out=result_of[blk][:, cols], in_=acc_of[blk, h][:])
                     else:
-                        nc.scalar.copy(out=result_of[blk][:, cols], in_=acc_of[blk][h][:])
-                        if h == 1:
-                            nc.sync.dma_start(out=out_blocks[blk], in_=result_of[blk][:])
+                        nc.vector.tensor_copy(out=result_of[blk][:, cols], in_=acc_of[blk, h][:])
+                    nc.sync.dma_start(out=out_blocks[blk][:, cols], in_=result_of[blk][:, cols])
+                else:
+                    nc.scalar.copy(out=result_of[blk][:, cols], in_=acc_of[blk, h][:])
+                    if h == 1:
+                        nc.sync.dma_start(out=out_blocks[blk], in_=result_of[blk][:])
+            blk, h = divmod(k - 5, 2)
+            if 0 <= blk < NB:
+                if blk == NB - 1 and h == 1:
+                    acc_of[blk, h] = q_psum.tile([P, N_TILE], F32, tag="q", name="last_acc")
+                else:
+                    acc_of[blk, h] = o_psum.tile([P, N_TILE], F32, name="acc")
+                for c in range(PASSES):
+                    nc.tensor.matmul_mx(
+                        out=acc_of[blk, h][:],
+                        lhsT=codes_of[PASSES * blk + c][0][:].bitcast(FP8X4),
+                        lhsT_scale=codes_of[PASSES * blk + c][1][:],
+                        rhs=w_codes[:, c, h * N_TILE : (h + 1) * N_TILE].bitcast(FP8X4),
+                        rhs_scale=w_scales[:, c, h * N_TILE : (h + 1) * N_TILE],
+                        start=(c == 0),
+                        stop=(c == PASSES - 1),
+                    )

@@ -25,7 +25,7 @@ FLOPS = 2 * N * M * COLS
 
 RELUS = (0, 1, 2, 3, 4, 5)
 CHAINS = ((6, 8, 10, 12, 14), (7, 9, 11, 13, 15))
-IN_PSUM = (8, 9, 10, 11)
+IN_PSUM = (8, 9, 10, 11, 12)
 BIG = 3.4028234663852886e38
 PLANE_ORDER = (6, 7, 0, 8, 9, 1, 10, 11, 2, 12, 13, 3, 14, 15, 4, 5)
 EARLY_PLANES = 3
@@ -40,7 +40,7 @@ def tile_tmk_kernel(tc, x, design_points, chol_inv, out):
         terms = stack.enter_context(tc.tile_pool(name="terms", bufs=27))
         work = stack.enter_context(tc.tile_pool(name="work", bufs=4))
         seeds = stack.enter_context(tc.tile_pool(name="seeds", bufs=1))
-        q_psum = stack.enter_context(tc.psum_pool(name="q_psum", bufs=3))
+        q_psum = stack.enter_context(tc.psum_pool(name="q_psum", bufs=2))
         o_psum = stack.enter_context(tc.psum_pool(name="o_psum", bufs=1))
         z_psum = stack.enter_context(tc.psum_pool(name="z_psum", bufs=1))
 
@@ -82,7 +82,7 @@ def tile_tmk_kernel(tc, x, design_points, chol_inv, out):
         def spread_planes(coordinates):
             for d in coordinates:
                 if d in IN_PSUM:
-                    plane = z_psum.tile([P, M], BF16, name="plane%d" % d)
+                    plane = z_psum.tile([P, M], BF16, tag="plane%d" % d, name="plane")
                 else:
                     plane = q_psum.tile([P, M], BF16, tag="q", name="plane")
                 for c in range(PASSES):
@@ -153,8 +153,7 @@ def tile_tmk_kernel(tc, x, design_points, chol_inv, out):
 
         def chain_ops(b, chains, first):
             ops = [(j, step) for step in range(1, len(CHAINS[0])) for j in range(len(CHAINS))]
-            half = len(ops) // 2
-            for j, step in ops[:half] if first else ops[half:]:
+            for j, step in ops[: len(IN_PSUM)] if first else ops[len(IN_PSUM) :]:
                 d = CHAINS[j][step]
                 if step == 1:
                     chains.append(terms.tile([P, M], F32, tag="term", name="chain"))
@@ -174,14 +173,48 @@ def tile_tmk_kernel(tc, x, design_points, chol_inv, out):
                     )
             return half_l1
 
-        def fold_late_half(tiles):
-            while len(tiles) > 1:
-                for i in range(0, len(tiles) - 1, 2):
-                    nc.vector.tensor_tensor(
-                        out=tiles[i][:, K_PASS:M], in0=tiles[i][:, K_PASS:M], in1=tiles[i + 1][:, K_PASS:M], op=ALU.add
-                    )
-                tiles = tiles[0::2]
-            return tiles
+        def add_pairs(tiles, cols):
+            for i in range(0, len(tiles) - 1, 2):
+                nc.vector.tensor_tensor(out=tiles[i][:, cols], in0=tiles[i][:, cols], in1=tiles[i + 1][:, cols], op=ALU.add)
+            return tiles[0::2]
+
+        def exponential(j):
+            grouped_of[j] = work.tile([P, P, PACK], BF16, align_bytes=64, name="k_grouped")
+            nc.scalar.activation(out=grouped_of[j][:], in_=half_of[j][:].rearrange("p t n -> p n t"), func=ACT.Exp, scale=-2.0)
+
+        def quantise(j):
+            k_codes = work.tile([P, P], U32, align_bytes=64, name="k_codes")
+            k_scales = work.tile([P, P], U8, align_bytes=64, name="k_scales")
+            nc.vector.quantize_mx(
+                out=k_codes[:].bitcast(FP8X4), scales=k_scales[:], in_=grouped_of[j][:].rearrange("p n t -> p (n t)")
+            )
+            codes_of[j] = (k_codes, k_scales)
+
+        def multiply(blk, h, c):
+            k_codes, k_scales = codes_of[PASSES * blk + c]
+            cols = slice(h * N_TILE, (h + 1) * N_TILE)
+            nc.tensor.matmul_mx(
+                out=acc_of[blk, h][:],
+                lhsT=k_codes[:].bitcast(FP8X4),
+                lhsT_scale=k_scales[:],
+                rhs=w_codes[:, c, cols].bitcast(FP8X4),
+                rhs_scale=w_scales[:, c, cols],
+                start=(c == 0),
+                stop=(c == PASSES - 1),
+            )
+
+        def copy_out(blk, h):
+            if h == 0:
+                result_of[blk] = work.tile([P, COLS], F32, name="result")
+            cols = slice(h * N_TILE, (h + 1) * N_TILE)
+            if blk >= NB - 3 and h == 1:
+                nc.vector.tensor_copy(out=result_of[blk][:, cols], in_=acc_of[blk, h][:])
+            else:
+                nc.scalar.copy(out=result_of[blk][:, cols], in_=acc_of[blk, h][:])
+            if blk == NB - 1:
+                nc.sync.dma_start(out=out_blocks[blk][:, cols], in_=result_of[blk][:, cols])
+            elif h == 1:
+                nc.sync.dma_start(out=out_blocks[blk], in_=result_of[blk][:])
 
         seeds_of = {0: make_seeds(0)}
         chains_of = {}
@@ -192,65 +225,85 @@ def tile_tmk_kernel(tc, x, design_points, chol_inv, out):
         acc_of = {}
         result_of = {}
         last = PASSES * NB
-        for k in range(-3, last + 9):
-            j = k - 2
-            if 0 <= j < last:
-                grouped_of[j] = work.tile([P, P, PACK], BF16, align_bytes=64, name="k_grouped")
-                nc.scalar.activation(
-                    out=grouped_of[j][:], in_=half_of[j][:].rearrange("p t n -> p n t"), func=ACT.Exp, scale=-2.0
-                )
-            j = k - 3
-            if 0 <= j < last:
-                k_codes = work.tile([P, P], U32, align_bytes=64, name="k_codes")
-                k_scales = work.tile([P, P], U8, align_bytes=64, name="k_scales")
-                nc.vector.quantize_mx(
-                    out=k_codes[:].bitcast(FP8X4), scales=k_scales[:], in_=grouped_of[j][:].rearrange("p n t -> p (n t)")
-                )
-                codes_of[j] = (k_codes, k_scales)
-            b, second = divmod(k + 3, 2)
-            if b < NB:
+        early, late = slice(0, K_PASS), slice(K_PASS, M)
+        pinned = {mybir.EngineType.DVE, mybir.EngineType.Activation, mybir.EngineType.PE, mybir.EngineType.Pool}
+        with tc.manual_schedule(engines=pinned):
+            for k in range(-3, last - 3):
+                b, second = divmod(k + 3, 2)
                 if second == 0:
                     chains_of[b] = []
                     relus_of[b] = []
+                    if b >= 3:
+                        quantise(PASSES * (b - 3))
+                        quantise(PASSES * (b - 3) + 1)
                 chain_ops(b, chains_of[b], second == 0)
                 if second == 0 and b + 1 < NB:
                     seeds_of[b + 1] = make_seeds(b + 1)
-                for d in RELUS[: n_relu // 2] if second == 0 else RELUS[n_relu // 2 :]:
+                if k == -2:
+                    quantise_weights()
+                mine = RELUS[: n_relu // 2] if second == 0 else RELUS[n_relu // 2 :]
+                for i, d in enumerate(mine):
                     relus_of[b].append(relu_term(b, d))
-            if k == -2:
-                quantise_weights()
-            if 0 <= k < last - 1:
-                half_of[k] = sum_terms([zr] + chains_of[k // 2] + relus_of[k // 2], k % 2)
-            if k == last - 1:
-                half_of[k] = sum_terms([zr] + fold_late_half(chains_of[k // 2] + relus_of[k // 2]), k % 2)
-            blk, h = divmod(k - 6, 2)
-            if 0 <= blk < NB:
-                if h == 0:
-                    result_of[blk] = work.tile([P, COLS], F32, name="result")
-                cols = slice(h * N_TILE, (h + 1) * N_TILE)
-                if blk == NB - 1:
-                    if h == 0:
-                        nc.scalar.copy(out=result_of[blk][:, cols], in_=acc_of[blk, h][:])
-                    else:
-                        nc.vector.tensor_copy(out=result_of[blk][:, cols], in_=acc_of[blk, h][:])
-                    nc.sync.dma_start(out=out_blocks[blk][:, cols], in_=result_of[blk][:, cols])
-                else:
-                    nc.scalar.copy(out=result_of[blk][:, cols], in_=acc_of[blk, h][:])
-                    if h == 1:
-                        nc.sync.dma_start(out=out_blocks[blk], in_=result_of[blk][:])
-            blk, h = divmod(k - 5, 2)
-            if 0 <= blk < NB:
-                if blk == NB - 1 and h == 1:
-                    acc_of[blk, h] = q_psum.tile([P, N_TILE], F32, tag="q", name="last_acc")
-                else:
+                    if i == 1 and k >= 1:
+                        exponential(k - 1)
+                if k >= 0:
+                    half_of[k] = sum_terms([zr] + chains_of[k // 2] + relus_of[k // 2], k % 2)
+                if k >= 5:
+                    copy_out(*divmod(k - 5, 2))
+                if k >= 4:
+                    blk, h = divmod(k - 4, 2)
                     acc_of[blk, h] = o_psum.tile([P, N_TILE], F32, name="acc")
+                    for c in range(PASSES):
+                        multiply(blk, h, c)
+
+            end = last - 3
+            quantise(end - 3)
+            exponential(end - 1)
+            quantise(end - 2)
+            half_of[end] = sum_terms([zr] + chains_of[end // 2] + relus_of[end // 2], end % 2)
+            tiles = chains_of[NB - 1] + relus_of[NB - 1]
+            early_tiles = add_pairs(tiles, early)
+            late_tiles = tiles
+            while len(late_tiles) > 1:
+                late_tiles = add_pairs(late_tiles, late)
+            copy_out(*divmod(end - 5, 2))
+            blk, h = divmod(end - 4, 2)
+            acc_of[blk, h] = o_psum.tile([P, N_TILE], F32, name="acc")
+            for c in range(PASSES):
+                multiply(blk, h, c)
+
+            exponential(end)
+            quantise(end - 1)
+            half_of[end + 1] = sum_terms([zr] + early_tiles, (end + 1) % 2)
+            copy_out(*divmod(end - 4, 2))
+            blk = NB - 3
+            acc_of[blk, 0] = o_psum.tile([P, N_TILE], F32, name="acc")
+            for c in range(PASSES):
+                multiply(blk, 0, c)
+
+            quantise(end)
+            exponential(end + 1)
+            half_of[end + 2] = sum_terms([zr] + late_tiles, (end + 2) % 2)
+            copy_out(blk, 0)
+            acc_of[blk, 1] = o_psum.tile([P, N_TILE], F32, name="acc")
+            for c in range(PASSES):
+                multiply(blk, 1, c)
+            quantise(end + 1)
+
+            free = ["plane%d" % d for d in IN_PSUM]
+            for blk in (NB - 2, NB - 1):
+                for h in range(COLS // N_TILE):
+                    acc_of[blk, h] = z_psum.tile([P, N_TILE], F32, tag=free.pop(0), name="late_acc")
+            exponential(end + 2)
+            quantise(end + 2)
+            for h in range(COLS // N_TILE):
                 for c in range(PASSES):
-                    nc.tensor.matmul_mx(
-                        out=acc_of[blk, h][:],
-                        lhsT=codes_of[PASSES * blk + c][0][:].bitcast(FP8X4),
-                        lhsT_scale=codes_of[PASSES * blk + c][1][:],
-                        rhs=w_codes[:, c, h * N_TILE : (h + 1) * N_TILE].bitcast(FP8X4),
-                        rhs_scale=w_scales[:, c, h * N_TILE : (h + 1) * N_TILE],
-                        start=(c == 0),
-                        stop=(c == PASSES - 1),
-                    )
+                    multiply(NB - 2, h, c)
+            copy_out(NB - 3, 1)
+            for h in range(COLS // N_TILE):
+                multiply(NB - 1, h, 0)
+            for h in range(COLS // N_TILE):
+                copy_out(NB - 2, h)
+            for h in range(COLS // N_TILE):
+                multiply(NB - 1, h, 1)
+                copy_out(NB - 1, h)

@@ -164,12 +164,12 @@ def tile_tmk_kernel(tc, x, design_points, chol_inv, out):
 
         def sum_terms(parts, c):
             half_l1 = q_psum.tile([P, PACK, P], F32, tag="q", name="half_l1")
-            for t in range(PACK):
-                lo = c * K_PASS + t * P
-                for i, part in enumerate(parts):
+            for i, part in enumerate(parts):
+                for t in range(PACK):
+                    lo = c * K_PASS + t * P
                     nc.tensor.matmul(
                         out=half_l1[:, t, :], lhsT=part[:, lo : lo + P], rhs=ident[:], is_transpose=True,
-                        start=(i == 0), stop=(i == len(parts) - 1),
+                        start=(i == 0 and t == 0), stop=(i == len(parts) - 1 and t == PACK - 1),
                     )
             return half_l1
 
@@ -207,7 +207,7 @@ def tile_tmk_kernel(tc, x, design_points, chol_inv, out):
             if h == 0:
                 result_of[blk] = work.tile([P, COLS], F32, name="result")
             cols = slice(h * N_TILE, (h + 1) * N_TILE)
-            if blk >= NB - 3 and h == 1:
+            if blk >= NB - 2 and h == 1:
                 nc.vector.tensor_copy(out=result_of[blk][:, cols], in_=acc_of[blk, h][:])
             else:
                 nc.scalar.copy(out=result_of[blk][:, cols], in_=acc_of[blk, h][:])
@@ -228,8 +228,8 @@ def tile_tmk_kernel(tc, x, design_points, chol_inv, out):
         early, late = slice(0, K_PASS), slice(K_PASS, M)
         pinned = {mybir.EngineType.DVE, mybir.EngineType.Activation, mybir.EngineType.PE, mybir.EngineType.Pool}
         with tc.manual_schedule(engines=pinned):
-            for k in range(-3, last - 3):
-                b, second = divmod(k + 3, 2)
+            for k in range(-2, last - 2):
+                b, second = divmod(k + 2, 2)
                 if second == 0:
                     chains_of[b] = []
                     relus_of[b] = []
@@ -239,7 +239,7 @@ def tile_tmk_kernel(tc, x, design_points, chol_inv, out):
                 chain_ops(b, chains_of[b], second == 0)
                 if second == 0 and b + 1 < NB:
                     seeds_of[b + 1] = make_seeds(b + 1)
-                if k == -2:
+                if k == -1:
                     quantise_weights()
                 mine = RELUS[: n_relu // 2] if second == 0 else RELUS[n_relu // 2 :]
                 for i, d in enumerate(mine):
@@ -247,7 +247,7 @@ def tile_tmk_kernel(tc, x, design_points, chol_inv, out):
                     if i == 1 and k >= 1:
                         exponential(k - 1)
                 if k >= 0:
-                    half_of[k] = sum_terms([zr] + chains_of[k // 2] + relus_of[k // 2], k % 2)
+                    half_of[k] = sum_terms([zr] + relus_of[k // 2] + chains_of[k // 2], k % 2)
                 if k >= 5:
                     copy_out(*divmod(k - 5, 2))
                 if k >= 4:
@@ -256,54 +256,38 @@ def tile_tmk_kernel(tc, x, design_points, chol_inv, out):
                     for c in range(PASSES):
                         multiply(blk, h, c)
 
-            end = last - 3
-            quantise(end - 3)
-            exponential(end - 1)
-            quantise(end - 2)
-            half_of[end] = sum_terms([zr] + chains_of[end // 2] + relus_of[end // 2], end % 2)
-            tiles = chains_of[NB - 1] + relus_of[NB - 1]
-            early_tiles = add_pairs(tiles, early)
-            late_tiles = tiles
-            while len(late_tiles) > 1:
-                late_tiles = add_pairs(late_tiles, late)
-            copy_out(*divmod(end - 5, 2))
-            blk, h = divmod(end - 4, 2)
-            acc_of[blk, h] = o_psum.tile([P, N_TILE], F32, name="acc")
-            for c in range(PASSES):
-                multiply(blk, h, c)
-
-            exponential(end)
-            quantise(end - 1)
-            half_of[end + 1] = sum_terms([zr] + early_tiles, (end + 1) % 2)
-            copy_out(*divmod(end - 4, 2))
-            blk = NB - 3
-            acc_of[blk, 0] = o_psum.tile([P, N_TILE], F32, name="acc")
-            for c in range(PASSES):
-                multiply(blk, 0, c)
-
-            quantise(end)
-            exponential(end + 1)
-            half_of[end + 2] = sum_terms([zr] + late_tiles, (end + 2) % 2)
-            copy_out(blk, 0)
-            acc_of[blk, 1] = o_psum.tile([P, N_TILE], F32, name="acc")
-            for c in range(PASSES):
-                multiply(blk, 1, c)
-            quantise(end + 1)
-
             free = ["plane%d" % d for d in IN_PSUM]
+            tiles = relus_of[NB - 1] + chains_of[NB - 1]
+            exponential(last - 3)
+            copy_out(*divmod(last - 7, 2))
+            quantise(last - 6)
+            quantise(last - 5)
+            early_tiles = add_pairs(tiles[:4], early) + tiles[4:]
+            acc_of[NB - 3, 0] = o_psum.tile([P, N_TILE], F32, name="acc")
+            acc_of[NB - 3, 1] = z_psum.tile([P, N_TILE], F32, tag=free.pop(0), name="late_acc")
+            for h in range(COLS // N_TILE):
+                for c in range(PASSES):
+                    multiply(NB - 3, h, c)
+                copy_out(NB - 3, h)
+            half_of[last - 2] = sum_terms([zr] + early_tiles, 0)
+            while len(tiles) > 1:
+                tiles = add_pairs(tiles, late)
+            exponential(last - 2)
+            half_of[last - 1] = sum_terms([zr] + tiles, 1)
+            quantise(last - 4)
+            quantise(last - 3)
+            quantise(last - 2)
+            exponential(last - 1)
+            quantise(last - 1)
             for blk in (NB - 2, NB - 1):
                 for h in range(COLS // N_TILE):
                     acc_of[blk, h] = z_psum.tile([P, N_TILE], F32, tag=free.pop(0), name="late_acc")
-            exponential(end + 2)
-            quantise(end + 2)
             for h in range(COLS // N_TILE):
                 for c in range(PASSES):
                     multiply(NB - 2, h, c)
-            copy_out(NB - 3, 1)
+                copy_out(NB - 2, h)
             for h in range(COLS // N_TILE):
                 multiply(NB - 1, h, 0)
-            for h in range(COLS // N_TILE):
-                copy_out(NB - 2, h)
             for h in range(COLS // N_TILE):
                 multiply(NB - 1, h, 1)
                 copy_out(NB - 1, h)

@@ -28,7 +28,7 @@ CHAINS = ((6, 8, 10, 12, 14), (7, 9, 11, 13, 15))
 IN_PSUM = (8, 9, 10, 11, 12)
 BIG = 3.4028234663852886e38
 PLANE_ORDER = (6, 7, 0, 8, 9, 1, 10, 11, 2, 12, 13, 3, 14, 15, 4, 5)
-EARLY_PLANES = 3
+EARLY_PLANES = 2
 
 
 def tile_tmk_kernel(tc, x, design_points, chol_inv, out):
@@ -67,13 +67,12 @@ def tile_tmk_kernel(tc, x, design_points, chol_inv, out):
         w_scales = keep.tile([P, PASSES, COLS], U8, align_bytes=64)
         xn = keep.tile([P, NB, D], F32)
 
-        xf = setup.tile([P, NB, D], F32)
-        nc.vector.tensor_copy(out=xf[:], in_=x_raw[:])
-        mean = setup.tile([P, NB], F32)
-        nc.vector.tensor_reduce(out=mean[:], in_=xf[:], axis=AX.X, op=ALU.add)
-        nc.vector.tensor_scalar_mul(out=mean[:], in0=mean[:], scalar1=1.0 / D)
+        total = setup.tile([P, NB], F32)
+        nc.vector.tensor_reduce(out=total[:], in_=x_raw[:], axis=AX.X, op=ALU.add)
         xc = setup.tile([P, NB, D], F32)
-        nc.vector.tensor_tensor(out=xc[:], in0=xf[:], in1=mean[:].unsqueeze(2).to_broadcast([P, NB, D]), op=ALU.subtract)
+        nc.vector.scalar_tensor_tensor(
+            out=xc[:], in0=total[:].unsqueeze(2).to_broadcast([P, NB, D]), scalar=-1.0 / D, in1=x_raw[:], op0=ALU.mult, op1=ALU.add
+        )
         sq = setup.tile([P, NB, D], F32)
         nc.vector.tensor_tensor(out=sq[:], in0=xc[:], in1=xc[:], op=ALU.mult)
         var = setup.tile([P, NB], F32)
@@ -88,25 +87,32 @@ def tile_tmk_kernel(tc, x, design_points, chol_inv, out):
                 for c in range(PASSES):
                     for t in range(PACK):
                         lo = c * K_PASS + t * P
-                        nc.tensor.transpose(plane[:, lo : lo + P], z_sb[:, c, t, d : d + 1].to_broadcast([P, P]), ident_bf[:])
+                        nc.tensor.matmul(
+                            out=plane[:, lo : lo + P], lhsT=z_sb[:, c, t, d : d + 1].to_broadcast([P, P]), rhs=ident_bf[:],
+                            start=True, stop=True,
+                        )
                 if d in IN_PSUM:
                     z_plane[d] = plane[:]
                 else:
                     nc.scalar.copy(out=zb[:, d, :], in_=plane[:])
                     z_plane[d] = zb[:, d, :]
 
+        one = setup.tile([P, 1], F32)
+        nc.vector.memset(one[:], 1.0)
         with tc.manual_schedule(engines={mybir.EngineType.Activation}):
+            nc.scalar.activation(out=one[:], in_=one[:], func=ACT.Abs_reciprocal_sqrt)
             spread_planes(PLANE_ORDER[:EARLY_PLANES])
-            std = setup.tile([P, NB], F32)
-            nc.scalar.activation(out=std[:], in_=var[:], func=ACT.Sqrt)
             rstd = setup.tile([P, NB], F32)
-            nc.vector.reciprocal(out=rstd[:], in_=std[:])
+            nc.scalar.activation(out=rstd[:], in_=var[:], func=ACT.Abs_reciprocal_sqrt)
             nt = setup.tile([P, NB], F32)
-            nc.vector.tensor_tensor(out=nt[:], in0=rstd[:], in1=rstd[:], op=ALU.mult)
+            nc.vector.scalar_tensor_tensor(out=nt[:], in0=rstd[:], scalar=-0.5, in1=rstd[:], op0=ALU.mult, op1=ALU.mult)
             nc.vector.tensor_tensor(out=nt[:], in0=nt[:], in1=var[:], op=ALU.mult)
-            nc.vector.tensor_scalar(out=nt[:], in0=nt[:], scalar1=-0.5, scalar2=1.5, op0=ALU.mult, op1=ALU.add)
-            nc.vector.tensor_tensor(out=rstd[:], in0=rstd[:], in1=nt[:], op=ALU.mult)
-            nc.vector.tensor_tensor(out=xn[:], in0=xc[:], in1=rstd[:].unsqueeze(2).to_broadcast([P, NB, D]), op=ALU.mult)
+            nc.vector.scalar_tensor_tensor(out=rstd[:], in0=nt[:], scalar=1.5, in1=rstd[:], op0=ALU.add, op1=ALU.mult)
+            for part in (slice(0, 2), slice(2, NB)):
+                n_part = part.stop - part.start
+                nc.vector.tensor_tensor(
+                    out=xn[:, part, :], in0=xc[:, part, :], in1=rstd[:, part].unsqueeze(2).to_broadcast([P, n_part, D]), op=ALU.mult
+                )
 
             spread_planes(PLANE_ORDER[EARLY_PLANES:])
         n_relu = len(RELUS)
@@ -126,7 +132,7 @@ def tile_tmk_kernel(tc, x, design_points, chol_inv, out):
         def quantise_weights():
             for c in range(PASSES):
                 w_grouped = setup.tile([P, COLS, PACK], BF16, name="w_grouped%d" % c, align_bytes=64)
-                nc.vector.tensor_copy(out=w_grouped[:], in_=w_raws[c][:].rearrange("p j w -> p w j"))
+                nc.vector.tensor_copy(out=w_grouped[:].rearrange("p (v i) j -> p v j i", i=PACK), in_=w_raws[c][:].rearrange("p j (v i) -> p v j i", i=PACK))
                 nc.vector.quantize_mx(
                     out=w_codes[:, c, :].bitcast(FP8X4),
                     scales=w_scales[:, c, :],

@@ -24,7 +24,8 @@ LN_EPS = 1e-5
 FLOPS = 2 * N * M * COLS
 
 RELUS = (0, 1, 2, 3, 4, 5)
-CHAINS = ((6, 8, 10, 12, 14), (7, 9, 11, 13, 15))
+LONE = 15
+CHAINS = ((6, 8, 10, 12, 14), (7, 9, 11, 13))
 IN_PSUM = (8, 9, 10, 11, 12)
 BIG = 3.4028234663852886e38
 PLANE_ORDER = (6, 7, 0, 8, 9, 1, 10, 11, 2, 12, 13, 3, 14, 15, 4, 5)
@@ -158,7 +159,7 @@ def tile_tmk_kernel(tc, x, design_points, chol_inv, out):
             return made
 
         def chain_ops(b, chains, first):
-            ops = [(j, step) for step in range(1, len(CHAINS[0])) for j in range(len(CHAINS))]
+            ops = [(j, step) for step in range(1, D) for j in range(len(CHAINS)) if step < len(CHAINS[j])]
             for j, step in ops[: len(IN_PSUM)] if first else ops[len(IN_PSUM) :]:
                 d = CHAINS[j][step]
                 if step == 1:
@@ -167,6 +168,16 @@ def tile_tmk_kernel(tc, x, design_points, chol_inv, out):
                 nc.vector.scalar_tensor_tensor(
                     out=chains[j][:], in0=z_plane[d], scalar=xn[:, b, d : d + 1], in1=before[:], op0=ALU.max, op1=ALU.add
                 )
+
+        def lone_term(b):
+            part = terms.tile([P, M], F32, tag="term", name="lone")
+            nc.vector.tensor_scalar(
+                out=part[:], in0=z_plane[LONE], scalar1=xn[:, b, LONE : LONE + 1], scalar2=None, op0=ALU.max
+            )
+            return part
+
+        def terms_of(b):
+            return relus_of[b][1:] + [lone_of[b]] + chains_of[b]
 
         def sum_terms(parts, c):
             half_l1 = q_psum.tile([P, PACK, P], F32, tag="q", name="half_l1")
@@ -223,6 +234,7 @@ def tile_tmk_kernel(tc, x, design_points, chol_inv, out):
                 nc.sync.dma_start(out=out_blocks[blk], in_=result_of[blk][:])
 
         seeds_of = {0: make_seeds(0)}
+        lone_of = {}
         chains_of = {}
         relus_of = {}
         half_of = {}
@@ -234,26 +246,33 @@ def tile_tmk_kernel(tc, x, design_points, chol_inv, out):
         early, late = slice(0, K_PASS), slice(K_PASS, M)
         pinned = {mybir.EngineType.DVE, mybir.EngineType.Activation, mybir.EngineType.PE, mybir.EngineType.Pool}
         with tc.manual_schedule(engines=pinned):
-            for k in range(-2, last - 2):
+            for k in range(-3, last - 2):
                 b, second = divmod(k + 2, 2)
-                if second == 0:
-                    chains_of[b] = []
-                    relus_of[b] = []
-                    if b >= 3:
-                        quantise(PASSES * (b - 3))
-                        quantise(PASSES * (b - 3) + 1)
-                chain_ops(b, chains_of[b], second == 0)
-                if second == 0 and b + 1 < NB:
-                    seeds_of[b + 1] = make_seeds(b + 1)
-                if k == -1:
-                    quantise_weights()
+                if b >= 0:
+                    if second == 0:
+                        if b >= 3:
+                            quantise(PASSES * (b - 3))
+                            quantise(PASSES * (b - 3) + 1)
+                        lone_of[b] = lone_term(b)
+                        chains_of[b] = []
+                    chain_ops(b, chains_of[b], second == 0)
+                    if second == 0:
+                        nc.gpsimd.tensor_tensor(out=lone_of[b][:], in0=lone_of[b][:], in1=relus_of[b][0][:], op=ALU.add)
+                        if b + 1 < NB:
+                            seeds_of[b + 1] = make_seeds(b + 1)
+                    if k == -1:
+                        quantise_weights()
+                b, second = divmod(k + 3, 2)
                 mine = RELUS[: n_relu // 2] if second == 0 else RELUS[n_relu // 2 :]
+                if b < NB and second == 0:
+                    relus_of[b] = []
                 for i, d in enumerate(mine):
-                    relus_of[b].append(relu_term(b, d))
+                    if b < NB:
+                        relus_of[b].append(relu_term(b, d))
                     if i == 1 and k >= 1:
                         exponential(k - 1)
                 if k >= 0:
-                    half_of[k] = sum_terms([zr] + relus_of[k // 2] + chains_of[k // 2], k % 2)
+                    half_of[k] = sum_terms([zr] + terms_of(k // 2), k % 2)
                 if k >= 5:
                     copy_out(*divmod(k - 5, 2))
                 if k >= 4:
@@ -263,7 +282,7 @@ def tile_tmk_kernel(tc, x, design_points, chol_inv, out):
                         multiply(blk, h, c)
 
             free = ["plane%d" % d for d in IN_PSUM]
-            tiles = relus_of[NB - 1] + chains_of[NB - 1]
+            tiles = terms_of(NB - 1)
             exponential(last - 3)
             copy_out(*divmod(last - 7, 2))
             quantise(last - 6)

@@ -24,11 +24,13 @@ LN_EPS = 1e-5
 FLOPS = 2 * N * M * COLS
 
 RELUS = (0, 1, 2, 3, 4, 5)
-LONE = 15
+LONES = (15,)
 CHAINS = ((6, 8, 10, 12, 14), (7, 9, 11, 13))
 IN_PSUM = (8, 9, 10, 11, 12)
 BIG = 3.4028234663852886e38
-PLANE_ORDER = (6, 7, 0, 8, 9, 1, 10, 11, 2, 12, 13, 3, 14, 15, 4, 5)
+PLANE_ORDER = (6, 7, 15, 0, 8, 9, 1, 10, 11, 2, 12, 13, 3, 14, 4, 5)
+SPLITS = 3
+ROWS = SPLITS * PACK
 EARLY_PLANES = 2
 
 
@@ -63,7 +65,9 @@ def tile_tmk_kernel(tc, x, design_points, chol_inv, out):
         make_identity(nc, ident_bf[:])
         zb = keep.tile([P, D, M], BF16)
         z_plane = {}
-        zr = keep.tile([P, M], F32)
+        zr_late = keep.tile([P, K_PASS], F32)
+        zr_rows = keep.tile([P, P], BF16)
+        zr_pick = [keep.tile([P, PACK, P], BF16, name="zr_pick%d" % c) for c in range(PASSES)]
         w_codes = keep.tile([P, PASSES, COLS], U32, align_bytes=64)
         w_scales = keep.tile([P, PASSES, COLS], U8, align_bytes=64)
         xn = keep.tile([P, NB, D], F32)
@@ -88,10 +92,7 @@ def tile_tmk_kernel(tc, x, design_points, chol_inv, out):
                 for c in range(PASSES):
                     for t in range(PACK):
                         lo = c * K_PASS + t * P
-                        nc.tensor.matmul(
-                            out=plane[:, lo : lo + P], lhsT=z_sb[:, c, t, d : d + 1].to_broadcast([P, P]), rhs=ident_bf[:],
-                            start=True, stop=True,
-                        )
+                        nc.tensor.transpose(plane[:, lo : lo + P], z_sb[:, c, t, d : d + 1].to_broadcast([P, P]), ident_bf[:])
                 if d in IN_PSUM:
                     z_plane[d] = plane[:]
                 else:
@@ -124,11 +125,32 @@ def tile_tmk_kernel(tc, x, design_points, chol_inv, out):
         z_rest = setup.tile([P, PASSES, PACK], F32)
         nc.vector.tensor_tensor(out=z_rest[:], in0=z_lo[:], in1=z_hi[:], op=ALU.subtract)
         nc.vector.tensor_scalar_mul(out=z_rest[:], in0=z_rest[:], scalar1=0.5)
+        rest = q_psum.tile([P, PACK, P], F32, tag="q", name="rest")
+        for t in range(PACK):
+            nc.tensor.transpose(rest[:, t, :], z_rest[:, 1, t : t + 1].to_broadcast([P, P]), ident[:])
+        nc.scalar.copy(out=zr_late[:], in_=rest[:].rearrange("p t q -> p (t q)"))
+        z_parts = setup.tile([P, P], BF16)
+        nc.gpsimd.memset(z_parts[:], 0.0)
         for c in range(PASSES):
-            rest = q_psum.tile([P, PACK, P], F32, tag="q", name="rest")
-            for t in range(PACK):
-                nc.tensor.transpose(rest[:, t, :], z_rest[:, c, t : t + 1].to_broadcast([P, P]), ident[:])
-            nc.scalar.copy(out=zr[:, c * K_PASS : (c + 1) * K_PASS], in_=rest[:].rearrange("p t q -> p (t q)"))
+            left = z_rest[:, c, :]
+            pick = setup.tile([P, PACK], F32, name="pick%d" % c)
+            for s in range(SPLITS):
+                rows = slice(ROWS * c + PACK * s, ROWS * c + PACK * (s + 1))
+                nc.gpsimd.tensor_copy(out=z_parts[:, rows], in_=left)
+                if s < SPLITS - 1:
+                    z_left = setup.tile([P, PACK], F32, name="z_left%d%d" % (c, s))
+                    nc.gpsimd.tensor_tensor(out=z_left[:], in0=left, in1=z_parts[:, rows], op=ALU.subtract)
+                    left = z_left[:]
+                if s == 0:
+                    nc.gpsimd.tensor_copy(out=pick[:], in_=ident[:, rows])
+                else:
+                    nc.gpsimd.tensor_tensor(out=pick[:], in0=pick[:], in1=ident[:, rows], op=ALU.add)
+            nc.gpsimd.tensor_scalar(
+                out=zr_pick[c][:], in0=pick[:].unsqueeze(2).to_broadcast([P, PACK, P]), scalar1=1.0, scalar2=0.0,
+                op0=ALU.mult, op1=ALU.add,
+            )
+        turned = q_psum.tile([P, P], BF16, tag="q", name="turned")
+        nc.tensor.transpose(turned[:], z_parts[:], ident_bf[:])
 
         def quantise_weights():
             for c in range(PASSES):
@@ -169,26 +191,36 @@ def tile_tmk_kernel(tc, x, design_points, chol_inv, out):
                     out=chains[j][:], in0=z_plane[d], scalar=xn[:, b, d : d + 1], in1=before[:], op0=ALU.max, op1=ALU.add
                 )
 
-        def lone_term(b):
+        def lone_term(b, d):
             part = terms.tile([P, M], F32, tag="term", name="lone")
-            nc.vector.tensor_scalar(
-                out=part[:], in0=z_plane[LONE], scalar1=xn[:, b, LONE : LONE + 1], scalar2=None, op0=ALU.max
-            )
+            nc.vector.tensor_scalar(out=part[:], in0=z_plane[d], scalar1=xn[:, b, d : d + 1], scalar2=None, op0=ALU.max)
             return part
 
         def terms_of(b):
-            return relus_of[b][1:] + [lone_of[b]] + chains_of[b]
+            return relus_of[b][1:] + lones_of[b] + chains_of[b]
 
-        def sum_terms(parts, c):
-            half_l1 = q_psum.tile([P, PACK, P], F32, tag="q", name="half_l1")
+        def constant_by_matmul(j):
+            blk, c = divmod(j, PASSES)
+            return c == 0 or blk % 5 % 2 == 0
+
+        def sum_terms(j, tiles):
+            half_of[j] = q_psum.tile([P, PACK, P], F32, tag="q", name="half_l1")
+            c = j % PASSES
+            parts = [part[:, c * K_PASS : (c + 1) * K_PASS] for part in tiles]
+            plain = constant_by_matmul(j)
+            if plain:
+                nc.tensor.matmul(
+                    out=half_of[j][:].rearrange("p t n -> p (t n)"), lhsT=zr_rows[:],
+                    rhs=zr_pick[c][:].rearrange("p t n -> p (t n)"), start=True, stop=False,
+                )
+            else:
+                parts = [zr_late[:]] + parts
             for i, part in enumerate(parts):
                 for t in range(PACK):
-                    lo = c * K_PASS + t * P
                     nc.tensor.matmul(
-                        out=half_l1[:, t, :], lhsT=part[:, lo : lo + P], rhs=ident[:], is_transpose=True,
-                        start=(i == 0 and t == 0), stop=(i == len(parts) - 1 and t == PACK - 1),
+                        out=half_of[j][:, t, :], lhsT=part[:, t * P : (t + 1) * P], rhs=ident[:], is_transpose=True,
+                        start=(not plain and i == 0 and t == 0), stop=(i == len(parts) - 1 and t == PACK - 1),
                     )
-            return half_l1
 
         def add_pairs(tiles, cols):
             for i in range(0, len(tiles) - 1, 2):
@@ -234,7 +266,7 @@ def tile_tmk_kernel(tc, x, design_points, chol_inv, out):
                 nc.sync.dma_start(out=out_blocks[blk], in_=result_of[blk][:])
 
         seeds_of = {0: make_seeds(0)}
-        lone_of = {}
+        lones_of = {}
         chains_of = {}
         relus_of = {}
         half_of = {}
@@ -253,14 +285,16 @@ def tile_tmk_kernel(tc, x, design_points, chol_inv, out):
                         if b >= 3:
                             quantise(PASSES * (b - 3))
                             quantise(PASSES * (b - 3) + 1)
-                        lone_of[b] = lone_term(b)
+                        lones_of[b] = [lone_term(b, d) for d in LONES]
                         chains_of[b] = []
                     chain_ops(b, chains_of[b], second == 0)
                     if second == 0:
-                        nc.gpsimd.tensor_tensor(out=lone_of[b][:], in0=lone_of[b][:], in1=relus_of[b][0][:], op=ALU.add)
+                        lone = lones_of[b][-1]
+                        nc.gpsimd.tensor_tensor(out=lone[:], in0=lone[:], in1=relus_of[b][0][:], op=ALU.add)
                         if b + 1 < NB:
                             seeds_of[b + 1] = make_seeds(b + 1)
                     if k == -1:
+                        nc.vector.tensor_copy(out=zr_rows[:], in_=turned[:])
                         quantise_weights()
                 b, second = divmod(k + 3, 2)
                 mine = RELUS[: n_relu // 2] if second == 0 else RELUS[n_relu // 2 :]
@@ -271,10 +305,10 @@ def tile_tmk_kernel(tc, x, design_points, chol_inv, out):
                         relus_of[b].append(relu_term(b, d))
                     if i == 1 and k >= 1:
                         exponential(k - 1)
-                if k >= 0:
-                    half_of[k] = sum_terms([zr] + terms_of(k // 2), k % 2)
                 if k >= 5:
                     copy_out(*divmod(k - 5, 2))
+                if k >= 0:
+                    sum_terms(k, terms_of(k // 2))
                 if k >= 4:
                     blk, h = divmod(k - 4, 2)
                     acc_of[blk, h] = o_psum.tile([P, N_TILE], F32, name="acc")
@@ -284,7 +318,7 @@ def tile_tmk_kernel(tc, x, design_points, chol_inv, out):
             free = ["plane%d" % d for d in IN_PSUM]
             tiles = terms_of(NB - 1)
             exponential(last - 3)
-            copy_out(*divmod(last - 7, 2))
+            copy_out(NB - 4, 1)
             quantise(last - 6)
             quantise(last - 5)
             early_tiles = add_pairs(tiles[:4], early) + tiles[4:]
@@ -294,11 +328,11 @@ def tile_tmk_kernel(tc, x, design_points, chol_inv, out):
                 for c in range(PASSES):
                     multiply(NB - 3, h, c)
                 copy_out(NB - 3, h)
-            half_of[last - 2] = sum_terms([zr] + early_tiles, 0)
+            sum_terms(last - 2, early_tiles)
             while len(tiles) > 1:
                 tiles = add_pairs(tiles, late)
             exponential(last - 2)
-            half_of[last - 1] = sum_terms([zr] + tiles, 1)
+            sum_terms(last - 1, tiles)
             quantise(last - 4)
             quantise(last - 3)
             quantise(last - 2)

@@ -25,6 +25,7 @@ FLOPS = 2 * N * M * COLS
 
 RELUS = (0, 1, 2, 3, 4, 5)
 LONES = (15,)
+MERGED = 768
 CHAINS = ((6, 8, 10, 12, 14), (7, 9, 11, 13))
 IN_PSUM = (8, 9, 10, 11, 12)
 BIG = 3.4028234663852886e38
@@ -43,6 +44,7 @@ def tile_tmk_kernel(tc, x, design_points, chol_inv, out):
         terms = stack.enter_context(tc.tile_pool(name="terms", bufs=27))
         work = stack.enter_context(tc.tile_pool(name="work", bufs=4))
         seeds = stack.enter_context(tc.tile_pool(name="seeds", bufs=1))
+        codes = stack.enter_context(tc.tile_pool(name="codes", bufs=6))
         q_psum = stack.enter_context(tc.psum_pool(name="q_psum", bufs=2))
         o_psum = stack.enter_context(tc.psum_pool(name="o_psum", bufs=1))
         z_psum = stack.enter_context(tc.psum_pool(name="z_psum", bufs=1))
@@ -106,6 +108,7 @@ def tile_tmk_kernel(tc, x, design_points, chol_inv, out):
             spread_planes(PLANE_ORDER[:EARLY_PLANES])
             rstd = setup.tile([P, NB], F32)
             nc.scalar.activation(out=rstd[:], in_=var[:], func=ACT.Abs_reciprocal_sqrt)
+            nc.scalar.activation(out=one[:], in_=one[:], func=ACT.Exp)
             nt = setup.tile([P, NB], F32)
             nc.vector.scalar_tensor_tensor(out=nt[:], in0=rstd[:], scalar=-0.5, in1=rstd[:], op0=ALU.mult, op1=ALU.mult)
             nc.vector.tensor_tensor(out=nt[:], in0=nt[:], in1=var[:], op=ALU.mult)
@@ -203,10 +206,13 @@ def tile_tmk_kernel(tc, x, design_points, chol_inv, out):
             blk, c = divmod(j, PASSES)
             return c == 0 or blk % 5 % 2 == 0
 
-        def sum_terms(j, tiles):
+        def sum_terms(j, tiles, unmerged=None):
             half_of[j] = q_psum.tile([P, PACK, P], F32, tag="q", name="half_l1")
             c = j % PASSES
-            parts = [part[:, c * K_PASS : (c + 1) * K_PASS] for part in tiles]
+            base = c * K_PASS
+            passes = [(part, base + t * P) for part in tiles for t in range(PACK)]
+            if unmerged is not None:
+                passes = [(unmerged, base + t * P) for t in range(PACK) if base + t * P >= MERGED] + passes
             plain = constant_by_matmul(j)
             if plain:
                 nc.tensor.matmul(
@@ -214,13 +220,13 @@ def tile_tmk_kernel(tc, x, design_points, chol_inv, out):
                     rhs=zr_pick[c][:].rearrange("p t n -> p (t n)"), start=True, stop=False,
                 )
             else:
-                parts = [zr_late[:]] + parts
-            for i, part in enumerate(parts):
-                for t in range(PACK):
-                    nc.tensor.matmul(
-                        out=half_of[j][:, t, :], lhsT=part[:, t * P : (t + 1) * P], rhs=ident[:], is_transpose=True,
-                        start=(not plain and i == 0 and t == 0), stop=(i == len(parts) - 1 and t == PACK - 1),
-                    )
+                passes = [(zr_late, base + t * P) for t in range(PACK)] + passes
+            for i, (part, lo) in enumerate(passes):
+                shift = K_PASS if part is zr_late else 0
+                nc.tensor.matmul(
+                    out=half_of[j][:, (lo - base) // P, :], lhsT=part[:, lo - shift : lo - shift + P], rhs=ident[:],
+                    is_transpose=True, start=(not plain and i == 0), stop=(i == len(passes) - 1),
+                )
 
         def add_pairs(tiles, cols):
             for i in range(0, len(tiles) - 1, 2):
@@ -228,12 +234,12 @@ def tile_tmk_kernel(tc, x, design_points, chol_inv, out):
             return tiles[0::2]
 
         def exponential(j):
-            grouped_of[j] = work.tile([P, P, PACK], BF16, align_bytes=64, name="k_grouped")
+            grouped_of[j] = codes.tile([P, P, PACK], BF16, align_bytes=64, name="k_grouped")
             nc.scalar.activation(out=grouped_of[j][:], in_=half_of[j][:].rearrange("p t n -> p n t"), func=ACT.Exp, scale=-2.0)
 
         def quantise(j):
-            k_codes = work.tile([P, P], U32, align_bytes=64, name="k_codes")
-            k_scales = work.tile([P, P], U8, align_bytes=64, name="k_scales")
+            k_codes = codes.tile([P, P], U32, align_bytes=64, name="k_codes")
+            k_scales = codes.tile([P, P], U8, align_bytes=64, name="k_scales")
             nc.vector.quantize_mx(
                 out=k_codes[:].bitcast(FP8X4), scales=k_scales[:], in_=grouped_of[j][:].rearrange("p n t -> p (n t)")
             )
@@ -256,7 +262,7 @@ def tile_tmk_kernel(tc, x, design_points, chol_inv, out):
             if h == 0:
                 result_of[blk] = work.tile([P, COLS], F32, name="result")
             cols = slice(h * N_TILE, (h + 1) * N_TILE)
-            if blk >= NB - 2 and h == 1:
+            if blk >= NB - 3 and h == 1:
                 nc.vector.tensor_copy(out=result_of[blk][:, cols], in_=acc_of[blk, h][:])
             else:
                 nc.scalar.copy(out=result_of[blk][:, cols], in_=acc_of[blk, h][:])
@@ -290,7 +296,8 @@ def tile_tmk_kernel(tc, x, design_points, chol_inv, out):
                     chain_ops(b, chains_of[b], second == 0)
                     if second == 0:
                         lone = lones_of[b][-1]
-                        nc.gpsimd.tensor_tensor(out=lone[:], in0=lone[:], in1=relus_of[b][0][:], op=ALU.add)
+                        cols = slice(0, M if b == NB - 1 else MERGED)
+                        nc.gpsimd.tensor_tensor(out=lone[:, cols], in0=lone[:, cols], in1=relus_of[b][0][:, cols], op=ALU.add)
                         if b + 1 < NB:
                             seeds_of[b + 1] = make_seeds(b + 1)
                     if k == -1:
@@ -308,7 +315,7 @@ def tile_tmk_kernel(tc, x, design_points, chol_inv, out):
                 if k >= 5:
                     copy_out(*divmod(k - 5, 2))
                 if k >= 0:
-                    sum_terms(k, terms_of(k // 2))
+                    sum_terms(k, terms_of(k // 2), relus_of[k // 2][0])
                 if k >= 4:
                     blk, h = divmod(k - 4, 2)
                     acc_of[blk, h] = o_psum.tile([P, N_TILE], F32, name="acc")
@@ -316,18 +323,18 @@ def tile_tmk_kernel(tc, x, design_points, chol_inv, out):
                         multiply(blk, h, c)
 
             free = ["plane%d" % d for d in IN_PSUM]
+            for blk in (NB - 3, NB - 2, NB - 1):
+                for h in range(COLS // N_TILE):
+                    if len(free) > 0:
+                        acc_of[blk, h] = z_psum.tile([P, N_TILE], F32, tag=free.pop(0), name="late_acc")
+                    else:
+                        acc_of[blk, h] = o_psum.tile([P, N_TILE], F32, name="acc")
             tiles = terms_of(NB - 1)
             exponential(last - 3)
             copy_out(NB - 4, 1)
             quantise(last - 6)
             quantise(last - 5)
             early_tiles = add_pairs(tiles[:4], early) + tiles[4:]
-            acc_of[NB - 3, 0] = o_psum.tile([P, N_TILE], F32, name="acc")
-            acc_of[NB - 3, 1] = z_psum.tile([P, N_TILE], F32, tag=free.pop(0), name="late_acc")
-            for h in range(COLS // N_TILE):
-                for c in range(PASSES):
-                    multiply(NB - 3, h, c)
-                copy_out(NB - 3, h)
             sum_terms(last - 2, early_tiles)
             while len(tiles) > 1:
                 tiles = add_pairs(tiles, late)
@@ -338,13 +345,11 @@ def tile_tmk_kernel(tc, x, design_points, chol_inv, out):
             quantise(last - 2)
             exponential(last - 1)
             quantise(last - 1)
-            for blk in (NB - 2, NB - 1):
+            for blk in (NB - 3, NB - 2):
                 for h in range(COLS // N_TILE):
-                    acc_of[blk, h] = z_psum.tile([P, N_TILE], F32, tag=free.pop(0), name="late_acc")
-            for h in range(COLS // N_TILE):
-                for c in range(PASSES):
-                    multiply(NB - 2, h, c)
-                copy_out(NB - 2, h)
+                    for c in range(PASSES):
+                        multiply(blk, h, c)
+                    copy_out(blk, h)
             for h in range(COLS // N_TILE):
                 multiply(NB - 1, h, 0)
             for h in range(COLS // N_TILE):

@@ -23,15 +23,15 @@ N_TILE = 512
 LN_EPS = 1e-5
 FLOPS = 2 * N * M * COLS
 
-RELUS = (0, 1, 2, 3, 4, 5)
-LONES = (15,)
-MERGED = 768
-CHAINS = ((6, 8, 10, 12, 14), (7, 9, 11, 13))
+USUAL = ((0, 1, 2, 3, 4, 5), (15,), (), ((6, 8, 10, 12, 14), (7, 9, 11, 13)))
+FIRST = ((0, 1, 2, 3, 4, 5), (15,), (13, 14), ((6, 8, 10, 12), (7, 9, 11)))
+FEWER = ((0, 1, 2, 3, 4), (15,), (), ((6, 8, 10, 12, 14), (7, 9, 11, 5, 13)))
+TURNED = 5
 IN_PSUM = (8, 9, 10, 11, 12)
+MERGED = 768
 BIG = 3.4028234663852886e38
-PLANE_ORDER = (6, 7, 15, 0, 8, 9, 1, 10, 11, 2, 12, 13, 3, 14, 4, 5)
+PLANE_ORDER = (6, 7, 15, 0, 8, 1, 9, 2, 10, 11, 13, 12, 14, 3, 4, 5)
 SPLITS = 3
-ROWS = SPLITS * PACK
 EARLY_PLANES = 2
 
 
@@ -67,9 +67,9 @@ def tile_tmk_kernel(tc, x, design_points, chol_inv, out):
         make_identity(nc, ident_bf[:])
         zb = keep.tile([P, D, M], BF16)
         z_plane = {}
-        zr_late = keep.tile([P, K_PASS], F32)
+        zr = keep.tile([P, M], F32)
         zr_rows = keep.tile([P, P], BF16)
-        zr_pick = [keep.tile([P, PACK, P], BF16, name="zr_pick%d" % c) for c in range(PASSES)]
+        zr_pick = keep.tile([P, PACK, P], BF16)
         w_codes = keep.tile([P, PASSES, COLS], U32, align_bytes=64)
         w_scales = keep.tile([P, PASSES, COLS], U8, align_bytes=64)
         xn = keep.tile([P, NB, D], F32)
@@ -85,6 +85,15 @@ def tile_tmk_kernel(tc, x, design_points, chol_inv, out):
         var = setup.tile([P, NB], F32)
         nc.vector.tensor_reduce(out=var[:], in_=sq[:], axis=AX.X, op=ALU.add)
         nc.vector.tensor_scalar(out=var[:], in0=var[:], scalar1=1.0 / D, scalar2=LN_EPS, op0=ALU.mult, op1=ALU.add)
+        def share(b):
+            return FIRST if b < 2 else FEWER if b % 8 == 4 else USUAL
+
+        def relu_term(b, d):
+            part = terms.tile([P, M], F32, tag="term", name="part")
+            nc.scalar.activation(out=part[:], in_=zb[:, d, :], func=ACT.Relu, bias=xn[:, b, d : d + 1], scale=-1.0)
+            return part
+
+        relus_of = {0: []}
         def spread_planes(coordinates):
             for d in coordinates:
                 if d in IN_PSUM:
@@ -94,12 +103,18 @@ def tile_tmk_kernel(tc, x, design_points, chol_inv, out):
                 for c in range(PASSES):
                     for t in range(PACK):
                         lo = c * K_PASS + t * P
-                        nc.tensor.transpose(plane[:, lo : lo + P], z_sb[:, c, t, d : d + 1].to_broadcast([P, P]), ident_bf[:])
+                        column = z_sb[:, c, t, d : d + 1].to_broadcast([P, P])
+                        if PLANE_ORDER.index(d) % 2 == 0:
+                            nc.tensor.matmul(out=plane[:, lo : lo + P], lhsT=column, rhs=ident_bf[:], start=True, stop=True)
+                        else:
+                            nc.tensor.transpose(plane[:, lo : lo + P], column, ident_bf[:])
                 if d in IN_PSUM:
                     z_plane[d] = plane[:]
                 else:
                     nc.scalar.copy(out=zb[:, d, :], in_=plane[:])
                     z_plane[d] = zb[:, d, :]
+                if d in share(0)[0]:
+                    relus_of[0].append(relu_term(0, d))
 
         one = setup.tile([P, 1], F32)
         nc.vector.memset(one[:], 1.0)
@@ -120,7 +135,7 @@ def tile_tmk_kernel(tc, x, design_points, chol_inv, out):
                 )
 
             spread_planes(PLANE_ORDER[EARLY_PLANES:])
-        n_relu = len(RELUS)
+        n_relu = len(USUAL[0])
         z_lo = setup.tile([P, PASSES, PACK], F32)
         nc.vector.tensor_reduce(out=z_lo[:], in_=z_sb[:, :, :, 0:n_relu], axis=AX.X, op=ALU.add)
         z_hi = setup.tile([P, PASSES, PACK], F32)
@@ -128,31 +143,30 @@ def tile_tmk_kernel(tc, x, design_points, chol_inv, out):
         z_rest = setup.tile([P, PASSES, PACK], F32)
         nc.vector.tensor_tensor(out=z_rest[:], in0=z_lo[:], in1=z_hi[:], op=ALU.subtract)
         nc.vector.tensor_scalar_mul(out=z_rest[:], in0=z_rest[:], scalar1=0.5)
-        rest = q_psum.tile([P, PACK, P], F32, tag="q", name="rest")
-        for t in range(PACK):
-            nc.tensor.transpose(rest[:, t, :], z_rest[:, 1, t : t + 1].to_broadcast([P, P]), ident[:])
-        nc.scalar.copy(out=zr_late[:], in_=rest[:].rearrange("p t q -> p (t q)"))
+        for c in range(PASSES):
+            rest = q_psum.tile([P, PACK, P], F32, tag="q", name="rest")
+            for t in range(PACK):
+                nc.tensor.transpose(rest[:, t, :], z_rest[:, c, t : t + 1].to_broadcast([P, P]), ident[:])
+            nc.scalar.copy(out=zr[:, c * K_PASS : (c + 1) * K_PASS], in_=rest[:].rearrange("p t q -> p (t q)"))
         z_parts = setup.tile([P, P], BF16)
         nc.gpsimd.memset(z_parts[:], 0.0)
-        for c in range(PASSES):
-            left = z_rest[:, c, :]
-            pick = setup.tile([P, PACK], F32, name="pick%d" % c)
-            for s in range(SPLITS):
-                rows = slice(ROWS * c + PACK * s, ROWS * c + PACK * (s + 1))
-                nc.gpsimd.tensor_copy(out=z_parts[:, rows], in_=left)
-                if s < SPLITS - 1:
-                    z_left = setup.tile([P, PACK], F32, name="z_left%d%d" % (c, s))
-                    nc.gpsimd.tensor_tensor(out=z_left[:], in0=left, in1=z_parts[:, rows], op=ALU.subtract)
-                    left = z_left[:]
-                if s == 0:
-                    nc.gpsimd.tensor_copy(out=pick[:], in_=ident[:, rows])
-                else:
-                    nc.gpsimd.tensor_tensor(out=pick[:], in0=pick[:], in1=ident[:, rows], op=ALU.add)
-            nc.gpsimd.tensor_scalar(
-                out=zr_pick[c][:], in0=pick[:].unsqueeze(2).to_broadcast([P, PACK, P]), scalar1=1.0, scalar2=0.0,
-                op0=ALU.mult, op1=ALU.add,
-            )
-        turned = q_psum.tile([P, P], BF16, tag="q", name="turned")
+        left = z_rest[:, 0, :]
+        pick = setup.tile([P, PACK], F32)
+        for s in range(SPLITS):
+            rows = slice(PACK * s, PACK * (s + 1))
+            nc.gpsimd.tensor_copy(out=z_parts[:, rows], in_=left)
+            if s < SPLITS - 1:
+                z_left = setup.tile([P, PACK], F32, name="z_left%d" % s)
+                nc.gpsimd.tensor_tensor(out=z_left[:], in0=left, in1=z_parts[:, rows], op=ALU.subtract)
+                left = z_left[:]
+            if s == 0:
+                nc.gpsimd.tensor_copy(out=pick[:], in_=ident[:, rows])
+            else:
+                nc.gpsimd.tensor_tensor(out=pick[:], in0=pick[:], in1=ident[:, rows], op=ALU.add)
+        nc.gpsimd.tensor_scalar(
+            out=zr_pick[:], in0=pick[:].unsqueeze(2).to_broadcast([P, PACK, P]), scalar1=1.0, scalar2=0.0, op0=ALU.mult, op1=ALU.add
+        )
+        turned = o_psum.tile([P, P], BF16, tag="acc", name="turned")
         nc.tensor.transpose(turned[:], z_parts[:], ident_bf[:])
 
         def quantise_weights():
@@ -165,14 +179,9 @@ def tile_tmk_kernel(tc, x, design_points, chol_inv, out):
                     in_=w_grouped[:].rearrange("p w j -> p (w j)"),
                 )
 
-        def relu_term(b, d):
-            part = terms.tile([P, M], F32, tag="term", name="part")
-            nc.scalar.activation(out=part[:], in_=zb[:, d, :], func=ACT.Relu, bias=xn[:, b, d : d + 1], scale=-1.0)
-            return part
-
         def make_seeds(b):
             made = []
-            for j, chain in enumerate(CHAINS):
+            for j, chain in enumerate(share(b)[3]):
                 d = chain[0]
                 seed = seeds.tile([P, M], F32, name="seed%d" % j)
                 x_col = xn[:, b, d : d + 1]
@@ -183,49 +192,61 @@ def tile_tmk_kernel(tc, x, design_points, chol_inv, out):
                 made.append(seed)
             return made
 
-        def chain_ops(b, chains, first):
-            ops = [(j, step) for step in range(1, D) for j in range(len(CHAINS)) if step < len(CHAINS[j])]
+        def chain_ops(b, first):
+            chains = share(b)[3]
+            ops = [(j, step) for step in range(1, D) for j in range(len(chains)) if step < len(chains[j])]
             for j, step in ops[: len(IN_PSUM)] if first else ops[len(IN_PSUM) :]:
-                d = CHAINS[j][step]
+                d = chains[j][step]
                 if step == 1:
-                    chains.append(terms.tile([P, M], F32, tag="term", name="chain"))
-                before = seeds_of[b][j] if step == 1 else chains[j]
+                    chains_of[b].append(terms.tile([P, M], F32, tag="term", name="chain"))
+                total_of = chains_of[b][j]
+                before = seeds_of[b][j] if step == 1 else total_of
+                turned_now = TURNED in (d, chains[j][step - 1])
                 nc.vector.scalar_tensor_tensor(
-                    out=chains[j][:], in0=z_plane[d], scalar=xn[:, b, d : d + 1], in1=before[:], op0=ALU.max, op1=ALU.add
+                    out=total_of[:], in0=z_plane[d], scalar=xn[:, b, d : d + 1], in1=before[:],
+                    op0=ALU.min if d == TURNED else ALU.max, op1=ALU.subtract if turned_now else ALU.add,
                 )
 
         def lone_term(b, d):
             part = terms.tile([P, M], F32, tag="term", name="lone")
-            nc.vector.tensor_scalar(out=part[:], in0=z_plane[d], scalar1=xn[:, b, d : d + 1], scalar2=None, op0=ALU.max)
+            x_col = xn[:, b, d : d + 1]
+            if TURNED in share(b)[0]:
+                nc.vector.tensor_scalar(out=part[:], in0=z_plane[d], scalar1=x_col, scalar2=None, op0=ALU.max)
+            else:
+                x_turned = xn[:, b, TURNED : TURNED + 1]
+                nc.vector.tensor_scalar(out=part[:], in0=z_plane[d], scalar1=x_col, scalar2=x_turned, op0=ALU.max, op1=ALU.add)
             return part
 
         def terms_of(b):
             return relus_of[b][1:] + lones_of[b] + chains_of[b]
 
         def constant_by_matmul(j):
-            blk, c = divmod(j, PASSES)
-            return c == 0 or blk % 5 % 2 == 0
+            return j % PASSES == 0 and j >= 2 * PASSES
 
-        def sum_terms(j, tiles, unmerged=None):
+        def sum_terms(j, first_tiles, later_tiles, unmerged=None):
             half_of[j] = q_psum.tile([P, PACK, P], F32, tag="q", name="half_l1")
             c = j % PASSES
-            base = c * K_PASS
-            passes = [(part, base + t * P) for part in tiles for t in range(PACK)]
-            if unmerged is not None:
-                passes = [(unmerged, base + t * P) for t in range(PACK) if base + t * P >= MERGED] + passes
             plain = constant_by_matmul(j)
             if plain:
                 nc.tensor.matmul(
                     out=half_of[j][:].rearrange("p t n -> p (t n)"), lhsT=zr_rows[:],
-                    rhs=zr_pick[c][:].rearrange("p t n -> p (t n)"), start=True, stop=False,
+                    rhs=zr_pick[:].rearrange("p t n -> p (t n)"), start=True, stop=False,
                 )
-            else:
-                passes = [(zr_late, base + t * P) for t in range(PACK)] + passes
-            for i, (part, lo) in enumerate(passes):
-                shift = K_PASS if part is zr_late else 0
+            passes = []
+            for t in range(PACK):
+                lo = c * K_PASS + t * P
+                if not plain:
+                    passes.append((t, zr[:, lo : lo + P]))
+                if unmerged is not None and lo >= MERGED:
+                    passes.append((t, unmerged[:, lo : lo + P]))
+                passes.extend([(t, part[:, lo : lo + P]) for part in first_tiles])
+            for t in range(PACK):
+                lo = c * K_PASS + t * P
+                passes.extend([(t, part[:, lo : lo + P]) for part in later_tiles])
+            for i, (t, chunk) in enumerate(passes):
                 nc.tensor.matmul(
-                    out=half_of[j][:, (lo - base) // P, :], lhsT=part[:, lo - shift : lo - shift + P], rhs=ident[:],
-                    is_transpose=True, start=(not plain and i == 0), stop=(i == len(passes) - 1),
+                    out=half_of[j][:, t, :], lhsT=chunk, rhs=ident[:], is_transpose=True,
+                    start=(not plain and i == 0), stop=(i == len(passes) - 1),
                 )
 
         def add_pairs(tiles, cols):
@@ -274,7 +295,6 @@ def tile_tmk_kernel(tc, x, design_points, chol_inv, out):
         seeds_of = {0: make_seeds(0)}
         lones_of = {}
         chains_of = {}
-        relus_of = {}
         half_of = {}
         grouped_of = {}
         codes_of = {}
@@ -291,34 +311,40 @@ def tile_tmk_kernel(tc, x, design_points, chol_inv, out):
                         if b >= 3:
                             quantise(PASSES * (b - 3))
                             quantise(PASSES * (b - 3) + 1)
-                        lones_of[b] = [lone_term(b, d) for d in LONES]
+                        lones_of[b] = [lone_term(b, d) for d in share(b)[1]]
                         chains_of[b] = []
-                    chain_ops(b, chains_of[b], second == 0)
+                    chain_ops(b, second == 0)
+                    if second == 1:
+                        lones_of[b].extend([lone_term(b, d) for d in share(b)[2]])
                     if second == 0:
-                        lone = lones_of[b][-1]
+                        lone = lones_of[b][0]
                         cols = slice(0, M if b == NB - 1 else MERGED)
                         nc.gpsimd.tensor_tensor(out=lone[:, cols], in0=lone[:, cols], in1=relus_of[b][0][:, cols], op=ALU.add)
                         if b + 1 < NB:
                             seeds_of[b + 1] = make_seeds(b + 1)
-                    if k == -1:
+                    if k == 1:
                         nc.vector.tensor_copy(out=zr_rows[:], in_=turned[:])
                         quantise_weights()
                 b, second = divmod(k + 3, 2)
-                mine = RELUS[: n_relu // 2] if second == 0 else RELUS[n_relu // 2 :]
-                if b < NB and second == 0:
-                    relus_of[b] = []
-                for i, d in enumerate(mine):
-                    if b < NB:
-                        relus_of[b].append(relu_term(b, d))
-                    if i == 1 and k >= 1:
-                        exponential(k - 1)
+                mine = ()
+                if 0 < b < NB:
+                    mine = share(b)[0][:3] if second == 0 else share(b)[0][3:]
+                    if second == 0:
+                        relus_of[b] = []
+                for d in mine[:2]:
+                    relus_of[b].append(relu_term(b, d))
+                if k >= 1:
+                    exponential(k - 1)
+                for d in mine[2:]:
+                    relus_of[b].append(relu_term(b, d))
                 if k >= 5:
                     copy_out(*divmod(k - 5, 2))
                 if k >= 0:
-                    sum_terms(k, terms_of(k // 2), relus_of[k // 2][0])
+                    blk = k // 2
+                    sum_terms(k, relus_of[blk][1:], lones_of[blk] + chains_of[blk], relus_of[blk][0])
                 if k >= 4:
                     blk, h = divmod(k - 4, 2)
-                    acc_of[blk, h] = o_psum.tile([P, N_TILE], F32, name="acc")
+                    acc_of[blk, h] = o_psum.tile([P, N_TILE], F32, tag="acc", name="acc")
                     for c in range(PASSES):
                         multiply(blk, h, c)
 
@@ -328,18 +354,17 @@ def tile_tmk_kernel(tc, x, design_points, chol_inv, out):
                     if len(free) > 0:
                         acc_of[blk, h] = z_psum.tile([P, N_TILE], F32, tag=free.pop(0), name="late_acc")
                     else:
-                        acc_of[blk, h] = o_psum.tile([P, N_TILE], F32, name="acc")
+                        acc_of[blk, h] = o_psum.tile([P, N_TILE], F32, tag="acc", name="acc")
             tiles = terms_of(NB - 1)
             exponential(last - 3)
             copy_out(NB - 4, 1)
             quantise(last - 6)
             quantise(last - 5)
-            early_tiles = add_pairs(tiles[:4], early) + tiles[4:]
-            sum_terms(last - 2, early_tiles)
+            sum_terms(last - 2, add_pairs(tiles, early), [])
             while len(tiles) > 1:
                 tiles = add_pairs(tiles, late)
             exponential(last - 2)
-            sum_terms(last - 1, tiles)
+            sum_terms(last - 1, tiles, [])
             quantise(last - 4)
             quantise(last - 3)
             quantise(last - 2)

@@ -28,7 +28,7 @@ FIRST = ((0, 1, 2, 3, 4, 5), (15,), (13, 14), ((6, 8, 10, 12), (7, 9, 11)))
 FEWER = ((0, 1, 2, 3, 4), (15,), (), ((6, 8, 10, 12, 14), (7, 9, 11, 5, 13)))
 TURNED = 5
 IN_PSUM = (8, 9, 10, 11, 12)
-MERGED = 768
+MERGED = 896
 BIG = 3.4028234663852886e38
 PLANE_ORDER = (6, 7, 15, 0, 8, 1, 9, 2, 10, 11, 13, 12, 14, 3, 4, 5)
 SPLITS = 3

from contextlib import ExitStack

import concourse.mybir as mybir
from concourse.masks import make_identity

F32 = mybir.dt.float32
BF16 = mybir.dt.bfloat16
U32 = mybir.dt.uint32
U8 = mybir.dt.uint8
FP8X4 = mybir.dt.float8_e4m3fn_x4
ALU = mybir.AluOpType
ACT = mybir.ActivationFunctionType
AX = mybir.AxisListType

P = 128
N, M, COLS, D = 4096, 1024, 1024, 16
NB = N // P
PACK = 4
K_PASS = P * PACK
PASSES = M // K_PASS
CT = PASSES * PACK
N_TILE = 512
LN_EPS = 1e-5
FLOPS = 2 * N * M * COLS

USUAL = ((0, 1, 2, 3, 4, 5), (15,), (), ((6, 8, 10, 12, 14), (7, 9, 11, 13)))
FIRST = ((0, 1, 2, 3, 4, 5), (15,), (13, 14), ((6, 8, 10, 12), (7, 9, 11)))
FEWER = ((0, 1, 2, 3, 4), (15,), (), ((6, 8, 10, 12, 14), (7, 9, 11, 5, 13)))
TURNED = 5
IN_PSUM = (8, 9, 10, 11, 12)
MERGED = 896
BIG = 3.4028234663852886e38
PLANE_ORDER = (6, 7, 15, 0, 8, 1, 9, 2, 10, 11, 13, 12, 14, 3, 4, 5)
SPLITS = 3
EARLY_PLANES = 2


def tile_tmk_kernel(tc, x, design_points, chol_inv, out):
    nc = tc.nc
    out_blocks = out.rearrange("(p b) c -> b p c", b=NB)
    with ExitStack() as stack:
        keep = stack.enter_context(tc.tile_pool(name="keep", bufs=1))
        setup = stack.enter_context(tc.tile_pool(name="setup", bufs=1))
        terms = stack.enter_context(tc.tile_pool(name="terms", bufs=27))
        work = stack.enter_context(tc.tile_pool(name="work", bufs=4))
        seeds = stack.enter_context(tc.tile_pool(name="seeds", bufs=1))
        codes = stack.enter_context(tc.tile_pool(name="codes", bufs=6))
        q_psum = stack.enter_context(tc.psum_pool(name="q_psum", bufs=2))
        o_psum = stack.enter_context(tc.psum_pool(name="o_psum", bufs=1))
        z_psum = stack.enter_context(tc.psum_pool(name="z_psum", bufs=1))

        x_raw = setup.tile([P, NB, D], BF16)
        nc.sync.dma_start(out=x_raw[:], in_=x.rearrange("(p b) d -> p b d", b=NB))
        z_sb = setup.tile([P, PASSES, PACK, D], BF16)
        nc.sync.dma_start(out=z_sb[:], in_=design_points.rearrange("(c q t) d -> q c t d", c=PASSES, t=PACK))
        w_raws = []
        for c in range(PASSES):
            w_raw = setup.tile([P, PACK, COLS], BF16, name="w_raw%d" % c)
            nc.sync.dma_start(
                out=w_raw[:], in_=chol_inv[c * K_PASS : (c + 1) * K_PASS, :].rearrange("(p j) w -> p j w", j=PACK)
            )
            w_raws.append(w_raw)

        ident = keep.tile([P, P], F32)
        make_identity(nc, ident[:])
        ident_bf = keep.tile([P, P], BF16)
        make_identity(nc, ident_bf[:])
        zb = keep.tile([P, D, M], BF16)
        z_plane = {}
        zr = keep.tile([P, M], F32)
        zr_rows = keep.tile([P, P], BF16)
        zr_pick = keep.tile([P, PACK, P], BF16)
        w_codes = keep.tile([P, PASSES, COLS], U32, align_bytes=64)
        w_scales = keep.tile([P, PASSES, COLS], U8, align_bytes=64)
        xn = keep.tile([P, NB, D], F32)

        total = setup.tile([P, NB], F32)
        nc.vector.tensor_reduce(out=total[:], in_=x_raw[:], axis=AX.X, op=ALU.add)
        xc = setup.tile([P, NB, D], F32)
        nc.vector.scalar_tensor_tensor(
            out=xc[:], in0=total[:].unsqueeze(2).to_broadcast([P, NB, D]), scalar=-1.0 / D, in1=x_raw[:], op0=ALU.mult, op1=ALU.add
        )
        sq = setup.tile([P, NB, D], F32)
        nc.vector.tensor_tensor(out=sq[:], in0=xc[:], in1=xc[:], op=ALU.mult)
        var = setup.tile([P, NB], F32)
        nc.vector.tensor_reduce(out=var[:], in_=sq[:], axis=AX.X, op=ALU.add)
        nc.vector.tensor_scalar(out=var[:], in0=var[:], scalar1=1.0 / D, scalar2=LN_EPS, op0=ALU.mult, op1=ALU.add)
        def share(b):
            return FIRST if b < 2 else FEWER if b % 8 == 4 else USUAL

        def relu_term(b, d):
            part = terms.tile([P, M], F32, tag="term", name="part")
            nc.scalar.activation(out=part[:], in_=zb[:, d, :], func=ACT.Relu, bias=xn[:, b, d : d + 1], scale=-1.0)
            return part

        relus_of = {0: []}
        def spread_planes(coordinates):
            for d in coordinates:
                if d in IN_PSUM:
                    plane = z_psum.tile([P, M], BF16, tag="plane%d" % d, name="plane")
                else:
                    plane = q_psum.tile([P, M], BF16, tag="q", name="plane")
                for c in range(PASSES):
                    for t in range(PACK):
                        lo = c * K_PASS + t * P
                        column = z_sb[:, c, t, d : d + 1].to_broadcast([P, P])
                        if PLANE_ORDER.index(d) % 2 == 0:
                            nc.tensor.matmul(out=plane[:, lo : lo + P], lhsT=column, rhs=ident_bf[:], start=True, stop=True)
                        else:
                            nc.tensor.transpose(plane[:, lo : lo + P], column, ident_bf[:])
                if d in IN_PSUM:
                    z_plane[d] = plane[:]
                else:
                    nc.scalar.copy(out=zb[:, d, :], in_=plane[:])
                    z_plane[d] = zb[:, d, :]
                if d in share(0)[0]:
                    relus_of[0].append(relu_term(0, d))

        one = setup.tile([P, 1], F32)
        nc.vector.memset(one[:], 1.0)
        with tc.manual_schedule(engines={mybir.EngineType.Activation}):
            nc.scalar.activation(out=one[:], in_=one[:], func=ACT.Abs_reciprocal_sqrt)
            spread_planes(PLANE_ORDER[:EARLY_PLANES])
            rstd = setup.tile([P, NB], F32)
            nc.scalar.activation(out=rstd[:], in_=var[:], func=ACT.Abs_reciprocal_sqrt)
            nc.scalar.activation(out=one[:], in_=one[:], func=ACT.Exp)
            nt = setup.tile([P, NB], F32)
            nc.vector.scalar_tensor_tensor(out=nt[:], in0=rstd[:], scalar=-0.5, in1=rstd[:], op0=ALU.mult, op1=ALU.mult)
            nc.vector.tensor_tensor(out=nt[:], in0=nt[:], in1=var[:], op=ALU.mult)
            nc.vector.scalar_tensor_tensor(out=rstd[:], in0=nt[:], scalar=1.5, in1=rstd[:], op0=ALU.add, op1=ALU.mult)
            for part in (slice(0, 2), slice(2, NB)):
                n_part = part.stop - part.start
                nc.vector.tensor_tensor(
                    out=xn[:, part, :], in0=xc[:, part, :], in1=rstd[:, part].unsqueeze(2).to_broadcast([P, n_part, D]), op=ALU.mult
                )

            spread_planes(PLANE_ORDER[EARLY_PLANES:])
        n_relu = len(USUAL[0])
        z_lo = setup.tile([P, PASSES, PACK], F32)
        nc.vector.tensor_reduce(out=z_lo[:], in_=z_sb[:, :, :, 0:n_relu], axis=AX.X, op=ALU.add)
        z_hi = setup.tile([P, PASSES, PACK], F32)
        nc.vector.tensor_reduce(out=z_hi[:], in_=z_sb[:, :, :, n_relu:D], axis=AX.X, op=ALU.add)
        z_rest = setup.tile([P, PASSES, PACK], F32)
        nc.vector.tensor_tensor(out=z_rest[:], in0=z_lo[:], in1=z_hi[:], op=ALU.subtract)
        nc.vector.tensor_scalar_mul(out=z_rest[:], in0=z_rest[:], scalar1=0.5)
        for c in range(PASSES):
            rest = q_psum.tile([P, PACK, P], F32, tag="q", name="rest")
            for t in range(PACK):
                nc.tensor.transpose(rest[:, t, :], z_rest[:, c, t : t + 1].to_broadcast([P, P]), ident[:])
            nc.scalar.copy(out=zr[:, c * K_PASS : (c + 1) * K_PASS], in_=rest[:].rearrange("p t q -> p (t q)"))
        z_parts = setup.tile([P, P], BF16)
        nc.gpsimd.memset(z_parts[:], 0.0)
        left = z_rest[:, 0, :]
        pick = setup.tile([P, PACK], F32)
        for s in range(SPLITS):
            rows = slice(PACK * s, PACK * (s + 1))
            nc.gpsimd.tensor_copy(out=z_parts[:, rows], in_=left)
            if s < SPLITS - 1:
                z_left = setup.tile([P, PACK], F32, name="z_left%d" % s)
                nc.gpsimd.tensor_tensor(out=z_left[:], in0=left, in1=z_parts[:, rows], op=ALU.subtract)
                left = z_left[:]
            if s == 0:
                nc.gpsimd.tensor_copy(out=pick[:], in_=ident[:, rows])
            else:
                nc.gpsimd.tensor_tensor(out=pick[:], in0=pick[:], in1=ident[:, rows], op=ALU.add)
        nc.gpsimd.tensor_scalar(
            out=zr_pick[:], in0=pick[:].unsqueeze(2).to_broadcast([P, PACK, P]), scalar1=1.0, scalar2=0.0, op0=ALU.mult, op1=ALU.add
        )
        turned = o_psum.tile([P, P], BF16, tag="acc", name="turned")
        nc.tensor.transpose(turned[:], z_parts[:], ident_bf[:])

        def quantise_weights():
            for c in range(PASSES):
                w_grouped = setup.tile([P, COLS, PACK], BF16, name="w_grouped%d" % c, align_bytes=64)
                nc.vector.tensor_copy(out=w_grouped[:].rearrange("p (v i) j -> p v j i", i=PACK), in_=w_raws[c][:].rearrange("p j (v i) -> p v j i", i=PACK))
                nc.vector.quantize_mx(
                    out=w_codes[:, c, :].bitcast(FP8X4),
                    scales=w_scales[:, c, :],
                    in_=w_grouped[:].rearrange("p w j -> p (w j)"),
                )

        def make_seeds(b):
            made = []
            for j, chain in enumerate(share(b)[3]):
                d = chain[0]
                seed = seeds.tile([P, M], F32, name="seed%d" % j)
                x_col = xn[:, b, d : d + 1]
                if b == 0:
                    nc.vector.tensor_scalar(out=seed[:], in0=z_plane[d], scalar1=x_col, scalar2=None, op0=ALU.max)
                else:
                    nc.gpsimd.tensor_scalar(out=seed[:], in0=z_plane[d], scalar1=BIG, scalar2=x_col, op0=ALU.min, op1=ALU.max)
                made.append(seed)
            return made

        def chain_ops(b, first):
            chains = share(b)[3]
            ops = [(j, step) for step in range(1, D) for j in range(len(chains)) if step < len(chains[j])]
            for j, step in ops[: len(IN_PSUM)] if first else ops[len(IN_PSUM) :]:
                d = chains[j][step]
                if step == 1:
                    chains_of[b].append(terms.tile([P, M], F32, tag="term", name="chain"))
                total_of = chains_of[b][j]
                before = seeds_of[b][j] if step == 1 else total_of
                turned_now = TURNED in (d, chains[j][step - 1])
                nc.vector.scalar_tensor_tensor(
                    out=total_of[:], in0=z_plane[d], scalar=xn[:, b, d : d + 1], in1=before[:],
                    op0=ALU.min if d == TURNED else ALU.max, op1=ALU.subtract if turned_now else ALU.add,
                )

        def lone_term(b, d):
            part = terms.tile([P, M], F32, tag="term", name="lone")
            x_col = xn[:, b, d : d + 1]
            if TURNED in share(b)[0]:
                nc.vector.tensor_scalar(out=part[:], in0=z_plane[d], scalar1=x_col, scalar2=None, op0=ALU.max)
            else:
                x_turned = xn[:, b, TURNED : TURNED + 1]
                nc.vector.tensor_scalar(out=part[:], in0=z_plane[d], scalar1=x_col, scalar2=x_turned, op0=ALU.max, op1=ALU.add)
            return part

        def terms_of(b):
            return relus_of[b][1:] + lones_of[b] + chains_of[b]

        def constant_by_matmul(j):
            return j % PASSES == 0 and j >= 2 * PASSES

        def sum_terms(j, first_tiles, later_tiles, unmerged=None):
            half_of[j] = q_psum.tile([P, PACK, P], F32, tag="q", name="half_l1")
            c = j % PASSES
            plain = constant_by_matmul(j)
            if plain:
                nc.tensor.matmul(
                    out=half_of[j][:].rearrange("p t n -> p (t n)"), lhsT=zr_rows[:],
                    rhs=zr_pick[:].rearrange("p t n -> p (t n)"), start=True, stop=False,
                )
            passes = []
            for t in range(PACK):
                lo = c * K_PASS + t * P
                if not plain:
                    passes.append((t, zr[:, lo : lo + P]))
                if unmerged is not None and lo >= MERGED:
                    passes.append((t, unmerged[:, lo : lo + P]))
                passes.extend([(t, part[:, lo : lo + P]) for part in first_tiles])
            for t in range(PACK):
                lo = c * K_PASS + t * P
                passes.extend([(t, part[:, lo : lo + P]) for part in later_tiles])
            for i, (t, chunk) in enumerate(passes):
                nc.tensor.matmul(
                    out=half_of[j][:, t, :], lhsT=chunk, rhs=ident[:], is_transpose=True,
                    start=(not plain and i == 0), stop=(i == len(passes) - 1),
                )

        def add_pairs(tiles, cols):
            for i in range(0, len(tiles) - 1, 2):
                nc.vector.tensor_tensor(out=tiles[i][:, cols], in0=tiles[i][:, cols], in1=tiles[i + 1][:, cols], op=ALU.add)
            return tiles[0::2]

        def exponential(j):
            grouped_of[j] = codes.tile([P, P, PACK], BF16, align_bytes=64, name="k_grouped")
            nc.scalar.activation(out=grouped_of[j][:], in_=half_of[j][:].rearrange("p t n -> p n t"), func=ACT.Exp, scale=-2.0)

        def quantise(j):
            k_codes = codes.tile([P, P], U32, align_bytes=64, name="k_codes")
            k_scales = codes.tile([P, P], U8, align_bytes=64, name="k_scales")
            nc.vector.quantize_mx(
                out=k_codes[:].bitcast(FP8X4), scales=k_scales[:], in_=grouped_of[j][:].rearrange("p n t -> p (n t)")
            )
            codes_of[j] = (k_codes, k_scales)

        def multiply(blk, h, c):
            k_codes, k_scales = codes_of[PASSES * blk + c]
            cols = slice(h * N_TILE, (h + 1) * N_TILE)
            nc.tensor.matmul_mx(
                out=acc_of[blk, h][:],
                lhsT=k_codes[:].bitcast(FP8X4),
                lhsT_scale=k_scales[:],
                rhs=w_codes[:, c, cols].bitcast(FP8X4),
                rhs_scale=w_scales[:, c, cols],
                start=(c == 0),
                stop=(c == PASSES - 1),
            )

        def copy_out(blk, h):
            if h == 0:
                result_of[blk] = work.tile([P, COLS], F32, name="result")
            cols = slice(h * N_TILE, (h + 1) * N_TILE)
            if blk >= NB - 3 and h == 1:
                nc.vector.tensor_copy(out=result_of[blk][:, cols], in_=acc_of[blk, h][:])
            else:
                nc.scalar.copy(out=result_of[blk][:, cols], in_=acc_of[blk, h][:])
            if blk == NB - 1:
                nc.sync.dma_start(out=out_blocks[blk][:, cols], in_=result_of[blk][:, cols])
            elif h == 1:
                nc.sync.dma_start(out=out_blocks[blk], in_=result_of[blk][:])

        seeds_of = {0: make_seeds(0)}
        lones_of = {}
        chains_of = {}
        half_of = {}
        grouped_of = {}
        codes_of = {}
        acc_of = {}
        result_of = {}
        last = PASSES * NB
        early, late = slice(0, K_PASS), slice(K_PASS, M)
        pinned = {mybir.EngineType.DVE, mybir.EngineType.Activation, mybir.EngineType.PE, mybir.EngineType.Pool}
        with tc.manual_schedule(engines=pinned):
            for k in range(-3, last - 2):
                b, second = divmod(k + 2, 2)
                if b >= 0:
                    if second == 0:
                        if b >= 3:
                            quantise(PASSES * (b - 3))
                            quantise(PASSES * (b - 3) + 1)
                        lones_of[b] = [lone_term(b, d) for d in share(b)[1]]
                        chains_of[b] = []
                    chain_ops(b, second == 0)
                    if second == 1:
                        lones_of[b].extend([lone_term(b, d) for d in share(b)[2]])
                    if second == 0:
                        lone = lones_of[b][0]
                        cols = slice(0, M if b == NB - 1 else MERGED)
                        nc.gpsimd.tensor_tensor(out=lone[:, cols], in0=lone[:, cols], in1=relus_of[b][0][:, cols], op=ALU.add)
                        if b + 1 < NB:
                            seeds_of[b + 1] = make_seeds(b + 1)
                    if k == 1:
                        nc.vector.tensor_copy(out=zr_rows[:], in_=turned[:])
                        quantise_weights()
                b, second = divmod(k + 3, 2)
                mine = ()
                if 0 < b < NB:
                    mine = share(b)[0][:3] if second == 0 else share(b)[0][3:]
                    if second == 0:
                        relus_of[b] = []
                for d in mine[:2]:
                    relus_of[b].append(relu_term(b, d))
                if k >= 1:
                    exponential(k - 1)
                for d in mine[2:]:
                    relus_of[b].append(relu_term(b, d))
                if k >= 5:
                    copy_out(*divmod(k - 5, 2))
                if k >= 0:
                    blk = k // 2
                    sum_terms(k, relus_of[blk][1:], lones_of[blk] + chains_of[blk], relus_of[blk][0])
                if k >= 4:
                    blk, h = divmod(k - 4, 2)
                    acc_of[blk, h] = o_psum.tile([P, N_TILE], F32, tag="acc", name="acc")
                    for c in range(PASSES):
                        multiply(blk, h, c)

            free = ["plane%d" % d for d in IN_PSUM]
            for blk in (NB - 3, NB - 2, NB - 1):
                for h in range(COLS // N_TILE):
                    if len(free) > 0:
                        acc_of[blk, h] = z_psum.tile([P, N_TILE], F32, tag=free.pop(0), name="late_acc")
                    else:
                        acc_of[blk, h] = o_psum.tile([P, N_TILE], F32, tag="acc", name="acc")
            tiles = terms_of(NB - 1)
            exponential(last - 3)
            copy_out(NB - 4, 1)
            quantise(last - 6)
            quantise(last - 5)
            sum_terms(last - 2, add_pairs(tiles, early), [])
            while len(tiles) > 1:
                tiles = add_pairs(tiles, late)
            exponential(last - 2)
            sum_terms(last - 1, tiles, [])
            quantise(last - 4)
            quantise(last - 3)
            quantise(last - 2)
            exponential(last - 1)
            quantise(last - 1)
            for blk in (NB - 3, NB - 2):
                for h in range(COLS // N_TILE):
                    for c in range(PASSES):
                        multiply(blk, h, c)
                    copy_out(blk, h)
            for h in range(COLS // N_TILE):
                multiply(NB - 1, h, 0)
            for h in range(COLS // N_TILE):
                multiply(NB - 1, h, 1)
                copy_out(NB - 1, h)
